import numpy as np
import ml_dtypes


def mxq(x, axis, fmt="e4m3"):
    dtype, down = {"e4m3": (ml_dtypes.float8_e4m3fn, 7), "e5m2": (ml_dtypes.float8_e5m2, 14)}[fmt]
    v = np.moveaxis(np.asarray(x, np.float32).astype(ml_dtypes.bfloat16).astype(np.float64), axis, -1)
    blocks = v.reshape(v.shape[:-1] + (-1, 32))
    amax = np.abs(blocks).max(-1, keepdims=True)
    byte = np.maximum(np.where(amax > 0, np.frexp(amax)[1] - 1 + 127, 0) - down, 1)
    scale = np.exp2(byte - 127.0)
    codes = (blocks / scale).astype(np.float32).astype(dtype).astype(np.float64)
    return np.moveaxis((codes * scale).reshape(v.shape), -1, axis)


WIDE = False


def mx_kscale(k):
    if not WIDE:
        return np.ones(k)
    levels = np.array([20, -20, 10, -10, 0])
    a = np.random.permutation(np.resize(levels, k // 512 * 4)).reshape(k // 512, 4)
    idx = np.arange(k)
    return np.exp2(a[idx // 512, idx % 128 // 32])


BF16 = ml_dtypes.bfloat16


def bf(x):
    return np.asarray(x, np.float32).astype(BF16)


def f64(x):
    return np.asarray(x).astype(np.float64)


B, C, HID, H, W = 2, 512, 256, 32, 16
N_P, N_H, N_F, N_U, N_L = 7, 3, 2, 4, 2
OU, OL = N_U * HID, N_L * HID
O = OU + OL
EPS = 1e-5


def conv_stats(xp, h_att, Wu, Wl):
    x = xp.reshape(B, C, H * W)
    a = h_att.reshape(N_H, B, 1, H * W)
    y = np.concatenate([Wu @ (a[1] * x), Wl @ (a[2] * x)], axis=1).reshape(B, O, H, W)
    m = y.mean(axis=(0, 2, 3))
    r = 1.0 / np.sqrt(y.var(axis=(0, 2, 3)) + EPS)
    return y, m, r


def setup_inputs():
    su = mx_kscale(OU)
    sl = mx_kscale(OL)
    off = 0.5 * np.random.standard_normal((1, C, 1, 1))
    p_nodes = bf(np.random.standard_normal((N_P, B, HID, H, W)))
    h_nodes = bf(np.random.standard_normal((N_H, B, HID, H, W)))
    f_nodes = bf(np.random.standard_normal((N_F, B, HID, H, W)))
    xp = bf(np.random.standard_normal((B, C, H, W)) + off)
    h_att = bf(np.random.uniform(0.0, 1.0, (N_H, B, 1, H, W)))
    Wu0 = bf(np.random.standard_normal((OU, C)) / np.sqrt(C))
    Wl0 = bf(np.random.standard_normal((OL, C)) / np.sqrt(C))
    gamma_u = bf(1.0 + 0.1 * np.random.standard_normal(OU))
    beta_u = bf(0.1 * np.random.standard_normal(OU))
    gamma_l = bf(1.0 + 0.1 * np.random.standard_normal(OL))
    beta_l = bf(0.1 * np.random.standard_normal(OL))
    sg = np.ones((N_P, 1, HID, 1, 1))
    sg[1:1 + N_U, 0, :, 0, 0] = su.reshape(N_U, HID)
    sg[1 + N_U:N_P, 0, :, 0, 0] = sl.reshape(N_L, HID)
    g = np.random.standard_normal((N_P, B, HID, H, W)) * np.exp2(np.random.randint(-12, 1, (1, B, 1, H, W))) * 16.0 * sg
    y, m, r = conv_stats(f64(xp), f64(h_att), f64(Wu0), f64(Wl0))
    return {
        "p_nodes": p_nodes,
        "h_nodes": h_nodes,
        "f_nodes": f_nodes,
        "xp": xp,
        "h_att": h_att,
        "Wu": bf(f64(Wu0) / su[:, None]),
        "Wl": bf(f64(Wl0) / sl[:, None]),
        "gamma_u": gamma_u,
        "beta_u": beta_u,
        "gamma_l": gamma_l,
        "beta_l": beta_l,
        "y": np.asarray(y, np.float32),
        "mean": np.asarray(m, np.float32),
        "rstd": np.asarray(r, np.float32),
        "grad_out": bf(g),
    }


def reference(p_nodes, h_nodes, f_nodes, xp, h_att, Wu, Wl, gamma_u, beta_u, gamma_l, beta_l, y, mean, rstd, grad_out):
    gamma = np.concatenate([f64(gamma_u), f64(gamma_l)])[None, :, None]
    beta = np.concatenate([f64(beta_u), f64(beta_l)])[None, :, None]
    r = f64(rstd)[None, :, None]
    xh = (f64(y).reshape(B, O, H * W) - f64(mean)[None, :, None]) * r
    g = f64(grad_out)[1:N_P].transpose(1, 0, 2, 3, 4).reshape(B, O, H * W)
    dh = 0.5 * g * (xh * gamma + beta > 0.0) * gamma
    m1 = dh.mean(axis=(0, 2), keepdims=True)
    m2 = (dh * xh).mean(axis=(0, 2), keepdims=True)
    dy = r * (dh - m1 - xh * m2)
    att = f64(h_att).reshape(N_H, B, 1, H * W)
    du = mxq(f64(Wu), 0, "e4m3").T @ mxq(dy[:, :OU], 1, "e5m2")
    dl = mxq(f64(Wl), 0, "e4m3").T @ mxq(dy[:, OU:], 1, "e5m2")
    return (att[1] * du + att[2] * dl).reshape(B, C, H, W)

@@ -1,0 +1,294 @@
+from contextlib import ExitStack
+
+import concourse.mybir as mybir
+from concourse.masks import make_identity
+
+F32 = mybir.dt.float32
+BF16 = mybir.dt.bfloat16
+U32 = mybir.dt.uint32
+U8 = mybir.dt.uint8
+E4M3X4 = mybir.dt.float8_e4m3fn_x4
+E5M2X4 = mybir.dt.float8_e5m2_x4
+ALU = mybir.AluOpType
+ACT = mybir.ActivationFunctionType
+
+P = 128
+PACK = 4
+BATCH = 2
+PIXELS = 512
+C_IN = 512
+UPPER_PASSES = 2
+PASSES = 3
+UNITS = PASSES * PACK
+PX_TILES = PIXELS // P
+C_TILES = C_IN // P
+VALUES = BATCH * PIXELS
+LOAD_AHEAD = 6
+
+ROW_GAMMA = 0
+ROW_BETA = ROW_GAMMA + UNITS
+ROW_ATT = ROW_BETA + UNITS
+ROW_F32 = 64
+ROW_MEAN = ROW_F32
+ROW_RSTD = ROW_MEAN + UNITS
+
+FLOPS = 2 * PASSES * PACK * P * C_IN * VALUES
+BYTES = (
+    UNITS * P * VALUES * (4 + 2)
+    + UNITS * P * C_IN * 2
+    + UNITS * P * (2 + 2 + 4 + 4)
+    + 2 * VALUES * 2
+    + C_IN * VALUES * 4
+)
+
+
+def by_fours_rows(ap):
+    return ap.rearrange("p t (c i) -> p c t i", i=PACK)
+
+
+def by_fours_words(ap):
+    return ap.rearrange("p (c i) t -> p c t i", i=PACK)
+
+
+def tile_gnn_t_v_kernel(
+    tc, p_nodes, h_nodes, f_nodes, xp, h_att, Wu, Wl, gamma_u, beta_u, gamma_l, beta_l, y, mean, rstd, grad_out, out
+):
+    nc = tc.nc
+    with ExitStack() as ctx:
+        keep = ctx.enter_context(tc.tile_pool(name="keep", bufs=1))
+        loads = ctx.enter_context(tc.tile_pool(name="loads", bufs=LOAD_AHEAD))
+        work = ctx.enter_context(tc.tile_pool(name="work", bufs=2))
+        psum = ctx.enter_context(tc.psum_pool(name="psum", bufs=8))
+
+        rows_bf16 = keep.tile([ROW_F32, P], BF16)
+        rows = keep.tile([P, P], F32)
+        nc.vector.memset(rows_bf16[:], 0.0)
+        nc.vector.memset(rows[ROW_F32:P, :], 0.0)
+        upper_units = UPPER_PASSES * PACK
+        for vec_u, vec_l, row in ((gamma_u, gamma_l, ROW_GAMMA), (beta_u, beta_l, ROW_BETA)):
+            nc.scalar.dma_start(out=rows_bf16[row : row + upper_units, :], in_=vec_u.rearrange("(r q) -> r q", q=P))
+            nc.scalar.dma_start(
+                out=rows_bf16[row + upper_units : row + UNITS, :], in_=vec_l.rearrange("(r q) -> r q", q=P)
+            )
+        nc.scalar.dma_start(out=rows[ROW_MEAN : ROW_MEAN + UNITS, :], in_=mean.rearrange("(r q) -> r q", q=P))
+        nc.scalar.dma_start(out=rows[ROW_RSTD : ROW_RSTD + UNITS, :], in_=rstd.rearrange("(r q) -> r q", q=P))
+        nc.scalar.dma_start(
+            out=rows_bf16[ROW_ATT : ROW_ATT + 2 * BATCH * PX_TILES, :],
+            in_=h_att[1:3].rearrange("i b o (j h) w -> (i b o j) (h w)", j=PX_TILES),
+        )
+        identity = keep.tile([P, P], F32)
+        make_identity(nc, identity[:])
+
+        w_views = [Wu.rearrange("(c t p) n -> c p t n", t=PACK, p=P)[c] for c in range(UPPER_PASSES)]
+        w_views.append(Wl.rearrange("(t p) n -> p t n", p=P))
+        w_raws = []
+        for c in range(PASSES):
+            w_raw = keep.tile([P, PACK, C_IN], BF16, name="w_raw%d" % c)
+            nc.sync.dma_start(out=w_raw[:], in_=w_views[c])
+            w_raws.append(w_raw)
+
+        y_view = y.rearrange("b (u p) h w -> u p b (h w)", p=P)
+        g_view = grad_out.rearrange("n b (v p) h w -> n v p b (h w)", p=P)
+        y_units = {}
+        g_units = {}
+
+        def load_unit(u):
+            y_unit = loads.tile([P, BATCH, PIXELS], F32)
+            nc.sync.dma_start(out=y_unit[:], in_=y_view[u])
+            g_unit = loads.tile([P, BATCH, PIXELS], BF16)
+            nc.sync.dma_start(out=g_unit[:], in_=g_view[1 + u // 2, u % 2])
+            y_units[u] = y_unit
+            g_units[u] = g_unit
+
+        for u in range(LOAD_AHEAD):
+            load_unit(u)
+
+        nc.vector.tensor_copy(out=rows[0:ROW_F32, :], in_=rows_bf16[:])
+        cols_psum = psum.tile([P, C_IN], F32, tag="bank")
+        nc.tensor.transpose(cols_psum[:, 0:P], rows[:], identity[:])
+        cols = keep.tile([P, P], F32)
+        nc.vector.tensor_copy(out=cols[:], in_=cols_psum[:, 0:P])
+        gamma = cols[:, ROW_GAMMA : ROW_GAMMA + UNITS]
+        beta = cols[:, ROW_BETA : ROW_BETA + UNITS]
+        mean_c = cols[:, ROW_MEAN : ROW_MEAN + UNITS]
+        rstd_c = cols[:, ROW_RSTD : ROW_RSTD + UNITS]
+
+        def att(i, b, j):
+            r = ROW_ATT + (i * BATCH + b) * PX_TILES + j
+            return cols[:, r : r + 1]
+
+        neg_beta = keep.tile([P, UNITS], F32)
+        nc.vector.tensor_scalar(out=neg_beta[:], in0=beta, scalar1=-1.0, scalar2=None, op0=ALU.mult)
+        neg_mean_rstd = keep.tile([P, UNITS], F32)
+        nc.vector.scalar_tensor_tensor(
+            out=neg_mean_rstd[:], in0=mean_c, scalar=-1.0, in1=rstd_c, op0=ALU.mult, op1=ALU.mult
+        )
+        half_gamma_rstd = keep.tile([P, UNITS], F32)
+        nc.vector.scalar_tensor_tensor(
+            out=half_gamma_rstd[:], in0=gamma, scalar=0.5, in1=rstd_c, op0=ALU.mult, op1=ALU.mult
+        )
+
+        w_codes = keep.tile([P, PASSES, C_IN], U32, align_bytes=64)
+        w_scales = keep.tile([P, PASSES, C_IN], U8, align_bytes=64)
+        w_words = {}
+        for c in range(PASSES + 1):
+            if c < PASSES:
+                w_word = work.tile([P, C_IN, PACK], BF16, align_bytes=64)
+                nc.vector.tensor_copy(out=by_fours_words(w_word[:]), in_=by_fours_rows(w_raws[c][:]))
+                w_words[c] = w_word
+            if c >= 1:
+                nc.vector.quantize_mx(
+                    out=w_codes[:, c - 1, :].bitcast(E4M3X4),
+                    scales=w_scales[:, c - 1, :],
+                    in_=w_words[c - 1][:].rearrange("p n t -> p (n t)"),
+                )
+
+        sum_e = keep.tile([P, UNITS], F32)
+        neg_mean_e = keep.tile([P, UNITS], F32)
+        neg_mean_e_xh = keep.tile([P, UNITS], F32)
+        xh_units = {}
+        masked_units = {}
+        e_passes = {}
+        corr_passes = {}
+
+        def normalise(u):
+            xh = work.tile([P, BATCH, PIXELS], F32, bufs=4)
+            nc.scalar.activation(
+                out=xh[:], in_=y_units[u][:], func=ACT.Identity,
+                scale=rstd_c[:, u : u + 1], bias=neg_mean_rstd[:, u : u + 1],
+            )
+            xh_units[u] = xh
+
+        def mask_gradient(u):
+            relu_on = work.tile([P, BATCH, PIXELS], BF16)
+            nc.vector.tensor_scalar(
+                out=relu_on[:], in0=xh_units[u][:], scalar1=gamma[:, u : u + 1], scalar2=neg_beta[:, u : u + 1],
+                op0=ALU.mult, op1=ALU.is_gt,
+            )
+            masked = work.tile([P, BATCH, PIXELS], BF16, bufs=3)
+            nc.vector.tensor_tensor(out=masked[:], in0=relu_on[:], in1=g_units[u][:], op=ALU.mult)
+            masked_units[u] = masked
+
+        def scale_gradient(u):
+            c, t = divmod(u, PACK)
+            if t == 0:
+                e_pass = work.tile([P, PACK, BATCH, PIXELS], F32)
+                e_passes[c] = e_pass
+            nc.scalar.activation(
+                out=e_passes[c][:, t], in_=masked_units[u][:], func=ACT.Copy,
+                scale=half_gamma_rstd[:, u : u + 1], accum_out=sum_e[:, u : u + 1],
+            )
+            nc.gpsimd.tensor_scalar(
+                out=neg_mean_e[:, u : u + 1], in0=sum_e[:, u : u + 1], scalar1=-1.0 / VALUES, scalar2=0.0,
+                op0=ALU.mult, op1=ALU.add,
+            )
+
+        def second_moment(u):
+            c, t = divmod(u, PACK)
+            product = work.tile([P, BATCH, PIXELS], BF16)
+            nc.vector.scalar_tensor_tensor(
+                out=product[:], in0=e_passes[c][:, t], scalar=-1.0 / VALUES, in1=xh_units[u][:],
+                op0=ALU.mult, op1=ALU.mult, accum_out=neg_mean_e_xh[:, u : u + 1],
+            )
+
+        def correction(u):
+            c, t = divmod(u, PACK)
+            if t == 0:
+                corr_pass = work.tile([P, PACK, BATCH, PIXELS], F32)
+                corr_passes[c] = corr_pass
+            nc.scalar.activation(
+                out=corr_passes[c][:, t], in_=xh_units[u][:], func=ACT.Identity,
+                scale=neg_mean_e_xh[:, u : u + 1], bias=neg_mean_e[:, u : u + 1],
+            )
+
+        dy_codes = keep.tile([P, PASSES, BATCH, PIXELS], U32, align_bytes=64)
+        dy_scales = keep.tile([P, PASSES, BATCH, PIXELS], U8, align_bytes=64)
+        upper = keep.tile([P, BATCH, PX_TILES, C_IN], F32)
+        sums = {}
+        out_view = out.rearrange("b (m p) h w -> b m p (h w)", p=P)
+
+        def quantise_pass(c):
+            dy_words = {}
+            for b in range(BATCH):
+                dy_word = work.tile([P, PIXELS, PACK], BF16, align_bytes=64)
+                nc.vector.tensor_tensor(
+                    out=by_fours_words(dy_word[:]),
+                    in0=by_fours_rows(e_passes[c][:, :, b, :]),
+                    in1=by_fours_rows(corr_passes[c][:, :, b, :]),
+                    op=ALU.add,
+                )
+                dy_words[b] = dy_word
+            for b in range(BATCH):
+                nc.vector.quantize_mx(
+                    out=dy_codes[:, c, b, :].bitcast(E5M2X4),
+                    scales=dy_scales[:, c, b, :],
+                    in_=dy_words[b][:].rearrange("p w t -> p (w t)"),
+                )
+
+        def multiply_pass(c, b, j, start, stop):
+            px = slice(j * P, (j + 1) * P)
+            nc.tensor.matmul_mx(
+                out=sums[(b, j)][:],
+                lhsT=dy_codes[:, c, b, px].bitcast(E5M2X4),
+                lhsT_scale=dy_scales[:, c, b, px],
+                rhs=w_codes[:, c, :].bitcast(E4M3X4),
+                rhs_scale=w_scales[:, c, :],
+                start=start,
+                stop=stop,
+            )
+
+        def finish_pass(c):
+            quantise_pass(c)
+            first = c == 0 or c == UPPER_PASSES
+            last = c == UPPER_PASSES - 1 or c == PASSES - 1
+            for b in range(BATCH):
+                for j in range(PX_TILES):
+                    if first:
+                        acc = psum.tile([P, C_IN], F32, tag="bank")
+                        sums[(b, j)] = acc
+                    multiply_pass(c, b, j, first, last)
+            if c == UPPER_PASSES - 1:
+                for b in range(BATCH):
+                    for j in range(PX_TILES):
+                        nc.scalar.activation(
+                            out=upper[:, b, j, :], in_=sums[(b, j)][:], func=ACT.Copy, scale=att(0, b, j)
+                        )
+            if c == PASSES - 1:
+                for b in range(BATCH):
+                    store_image(b)
+
+        def store_image(b):
+            by_pixel = []
+            for j in range(PX_TILES):
+                total = work.tile([P, C_IN], F32, bufs=2 * PX_TILES)
+                nc.vector.scalar_tensor_tensor(
+                    out=total[:], in0=sums[(b, j)][:], scalar=att(1, b, j), in1=upper[:, b, j, :],
+                    op0=ALU.mult, op1=ALU.add,
+                )
+                by_pixel.append(total)
+            for m in range(C_TILES):
+                turned = psum.tile([P, PIXELS], F32, tag="bank")
+                for j in range(PX_TILES):
+                    nc.tensor.transpose(
+                        turned[:, j * P : (j + 1) * P], by_pixel[j][:, m * P : (m + 1) * P], identity[:]
+                    )
+                result = work.tile([P, PIXELS], F32, bufs=4)
+                nc.scalar.copy(out=result[:], in_=turned[:])
+                nc.sync.dma_start(out=out_view[b, m], in_=result[:])
+
+        normalise(0)
+        for i in range(UNITS + 2):
+            if i + 1 < UNITS:
+                normalise(i + 1)
+            if i < UNITS:
+                mask_gradient(i)
+            if i >= 2 and (i - 2) % PACK == PACK - 1:
+                finish_pass((i - 2) // PACK)
+            if 1 <= i <= UNITS:
+                second_moment(i - 1)
+            if i < UNITS:
+                scale_gradient(i)
+            if 1 <= i <= UNITS:
+                correction(i - 1)
+            if i + LOAD_AHEAD < UNITS:
+                load_unit(i + LOAD_AHEAD)

@@ -23,7 +23,11 @@ UNITS = PASSES * PACK
 PX_TILES = PIXELS // P
 C_TILES = C_IN // P
 VALUES = BATCH * PIXELS
-LOAD_AHEAD = 6
+LOAD_AHEAD = 8
+
+FIRST_HALF_STEP = 6
+STEPS_PER_HALF = 2
+WEIGHT_STEP = 3
 
 ROW_GAMMA = 0
 ROW_BETA = ROW_GAMMA + UNITS
@@ -32,7 +36,7 @@ ROW_F32 = 64
 ROW_MEAN = ROW_F32
 ROW_RSTD = ROW_MEAN + UNITS
 
-FLOPS = 2 * PASSES * PACK * P * C_IN * VALUES
+FLOPS = 2 * UNITS * P * C_IN * VALUES
 BYTES = (
     UNITS * P * VALUES * (4 + 2)
     + UNITS * P * C_IN * 2
@@ -59,19 +63,20 @@ def tile_gnn_t_v_kernel(
         loads = ctx.enter_context(tc.tile_pool(name="loads", bufs=LOAD_AHEAD))
         work = ctx.enter_context(tc.tile_pool(name="work", bufs=2))
         psum = ctx.enter_context(tc.psum_pool(name="psum", bufs=8))
+        ctx.enter_context(tc.manual_schedule())
 
         rows_bf16 = keep.tile([ROW_F32, P], BF16)
         rows = keep.tile([P, P], F32)
         nc.vector.memset(rows_bf16[:], 0.0)
         nc.vector.memset(rows[ROW_F32:P, :], 0.0)
         upper_units = UPPER_PASSES * PACK
+        nc.scalar.dma_start(out=rows[ROW_MEAN : ROW_MEAN + UNITS, :], in_=mean.rearrange("(r q) -> r q", q=P))
+        nc.scalar.dma_start(out=rows[ROW_RSTD : ROW_RSTD + UNITS, :], in_=rstd.rearrange("(r q) -> r q", q=P))
         for vec_u, vec_l, row in ((gamma_u, gamma_l, ROW_GAMMA), (beta_u, beta_l, ROW_BETA)):
             nc.scalar.dma_start(out=rows_bf16[row : row + upper_units, :], in_=vec_u.rearrange("(r q) -> r q", q=P))
             nc.scalar.dma_start(
                 out=rows_bf16[row + upper_units : row + UNITS, :], in_=vec_l.rearrange("(r q) -> r q", q=P)
             )
-        nc.scalar.dma_start(out=rows[ROW_MEAN : ROW_MEAN + UNITS, :], in_=mean.rearrange("(r q) -> r q", q=P))
-        nc.scalar.dma_start(out=rows[ROW_RSTD : ROW_RSTD + UNITS, :], in_=rstd.rearrange("(r q) -> r q", q=P))
         nc.scalar.dma_start(
             out=rows_bf16[ROW_ATT : ROW_ATT + 2 * BATCH * PX_TILES, :],
             in_=h_att[1:3].rearrange("i b o (j h) w -> (i b o j) (h w)", j=PX_TILES),
@@ -81,11 +86,12 @@ def tile_gnn_t_v_kernel(
 
         w_views = [Wu.rearrange("(c t p) n -> c p t n", t=PACK, p=P)[c] for c in range(UPPER_PASSES)]
         w_views.append(Wl.rearrange("(t p) n -> p t n", p=P))
-        w_raws = []
-        for c in range(PASSES):
+        w_raws = {}
+
+        def load_weights(c):
             w_raw = keep.tile([P, PACK, C_IN], BF16, name="w_raw%d" % c)
             nc.sync.dma_start(out=w_raw[:], in_=w_views[c])
-            w_raws.append(w_raw)
+            w_raws[c] = w_raw
 
         y_view = y.rearrange("b (u p) h w -> u p b (h w)", p=P)
         g_view = grad_out.rearrange("n b (v p) h w -> n v p b (h w)", p=P)
@@ -102,6 +108,8 @@ def tile_gnn_t_v_kernel(
 
         for u in range(LOAD_AHEAD):
             load_unit(u)
+            if 0 <= u - (WEIGHT_STEP - 1) < PASSES:
+                load_weights(u - (WEIGHT_STEP - 1))
 
         nc.vector.tensor_copy(out=rows[0:ROW_F32, :], in_=rows_bf16[:])
         cols_psum = psum.tile([P, C_IN], F32, tag="bank")
@@ -117,150 +125,150 @@ def tile_gnn_t_v_kernel(
             r = ROW_ATT + (i * BATCH + b) * PX_TILES + j
             return cols[:, r : r + 1]
 
-        neg_beta = keep.tile([P, UNITS], F32)
-        nc.vector.tensor_scalar(out=neg_beta[:], in0=beta, scalar1=-1.0, scalar2=None, op0=ALU.mult)
-        neg_mean_rstd = keep.tile([P, UNITS], F32)
+        z_slope = keep.tile([P, UNITS], F32)
+        nc.vector.tensor_tensor(out=z_slope[:], in0=rstd_c, in1=gamma, op=ALU.mult)
+        mean_z_slope = keep.tile([P, UNITS], F32)
+        nc.vector.tensor_tensor(out=mean_z_slope[:], in0=mean_c, in1=z_slope[:], op=ALU.mult)
+        z_thresh = keep.tile([P, UNITS], F32)
+        nc.vector.tensor_tensor(out=z_thresh[:], in0=mean_z_slope[:], in1=beta, op=ALU.subtract)
+        e_scale = keep.tile([P, UNITS], F32)
+        nc.vector.tensor_scalar(out=e_scale[:], in0=z_slope[:], scalar1=0.5, scalar2=None, op0=ALU.mult)
+        rstd_sq = keep.tile([P, UNITS], F32)
+        nc.vector.tensor_tensor(out=rstd_sq[:], in0=rstd_c, in1=rstd_c, op=ALU.mult)
+        k_slope = keep.tile([P, UNITS], F32)
         nc.vector.scalar_tensor_tensor(
-            out=neg_mean_rstd[:], in0=mean_c, scalar=-1.0, in1=rstd_c, op0=ALU.mult, op1=ALU.mult
+            out=k_slope[:], in0=rstd_sq[:], scalar=-1.0 / VALUES, in1=e_scale[:], op0=ALU.mult, op1=ALU.mult
         )
-        half_gamma_rstd = keep.tile([P, UNITS], F32)
+        k_offset = keep.tile([P, UNITS], F32)
         nc.vector.scalar_tensor_tensor(
-            out=half_gamma_rstd[:], in0=gamma, scalar=0.5, in1=rstd_c, op0=ALU.mult, op1=ALU.mult
+            out=k_offset[:], in0=k_slope[:], scalar=-1.0, in1=mean_c, op0=ALU.mult, op1=ALU.mult
         )
 
         w_codes = keep.tile([P, PASSES, C_IN], U32, align_bytes=64)
         w_scales = keep.tile([P, PASSES, C_IN], U8, align_bytes=64)
         w_words = {}
-        for c in range(PASSES + 1):
-            if c < PASSES:
-                w_word = work.tile([P, C_IN, PACK], BF16, align_bytes=64)
-                nc.vector.tensor_copy(out=by_fours_words(w_word[:]), in_=by_fours_rows(w_raws[c][:]))
-                w_words[c] = w_word
-            if c >= 1:
-                nc.vector.quantize_mx(
-                    out=w_codes[:, c - 1, :].bitcast(E4M3X4),
-                    scales=w_scales[:, c - 1, :],
-                    in_=w_words[c - 1][:].rearrange("p n t -> p (n t)"),
-                )
 
+        def regroup_weights(c):
+            w_word = work.tile([P, C_IN, PACK], BF16, bufs=PASSES, align_bytes=64)
+            nc.scalar.copy(out=by_fours_words(w_word[:]), in_=by_fours_rows(w_raws[c][:]))
+            w_words[c] = w_word
+
+        def quantise_weights(c):
+            nc.vector.quantize_mx(
+                out=w_codes[:, c, :].bitcast(E4M3X4),
+                scales=w_scales[:, c, :],
+                in_=w_words[c][:].rearrange("p n t -> p (n t)"),
+            )
+
+        sum_cm = keep.tile([P, UNITS], F32)
         sum_e = keep.tile([P, UNITS], F32)
         neg_mean_e = keep.tile([P, UNITS], F32)
-        neg_mean_e_xh = keep.tile([P, UNITS], F32)
-        xh_units = {}
+        slope = keep.tile([P, UNITS], F32)
+        offset = keep.tile([P, UNITS], F32)
         masked_units = {}
         e_passes = {}
         corr_passes = {}
 
-        def normalise(u):
-            xh = work.tile([P, BATCH, PIXELS], F32, bufs=4)
-            nc.scalar.activation(
-                out=xh[:], in_=y_units[u][:], func=ACT.Identity,
-                scale=rstd_c[:, u : u + 1], bias=neg_mean_rstd[:, u : u + 1],
-            )
-            xh_units[u] = xh
-
-        def mask_gradient(u):
+        def mask_and_sum(u):
+            one = slice(u, u + 1)
             relu_on = work.tile([P, BATCH, PIXELS], BF16)
             nc.vector.tensor_scalar(
-                out=relu_on[:], in0=xh_units[u][:], scalar1=gamma[:, u : u + 1], scalar2=neg_beta[:, u : u + 1],
+                out=relu_on[:], in0=y_units[u][:], scalar1=z_slope[:, one], scalar2=z_thresh[:, one],
                 op0=ALU.mult, op1=ALU.is_gt,
             )
             masked = work.tile([P, BATCH, PIXELS], BF16, bufs=3)
             nc.vector.tensor_tensor(out=masked[:], in0=relu_on[:], in1=g_units[u][:], op=ALU.mult)
             masked_units[u] = masked
+            product = work.tile([P, BATCH, PIXELS], BF16)
+            nc.vector.scalar_tensor_tensor(
+                out=product[:], in0=y_units[u][:], scalar=mean_c[:, one], in1=masked[:],
+                op0=ALU.subtract, op1=ALU.mult, accum_out=sum_cm[:, one],
+            )
 
         def scale_gradient(u):
             c, t = divmod(u, PACK)
+            one = slice(u, u + 1)
             if t == 0:
                 e_pass = work.tile([P, PACK, BATCH, PIXELS], F32)
                 e_passes[c] = e_pass
             nc.scalar.activation(
                 out=e_passes[c][:, t], in_=masked_units[u][:], func=ACT.Copy,
-                scale=half_gamma_rstd[:, u : u + 1], accum_out=sum_e[:, u : u + 1],
+                scale=e_scale[:, one], accum_out=sum_e[:, one],
             )
             nc.gpsimd.tensor_scalar(
-                out=neg_mean_e[:, u : u + 1], in0=sum_e[:, u : u + 1], scalar1=-1.0 / VALUES, scalar2=0.0,
+                out=neg_mean_e[:, one], in0=sum_e[:, one], scalar1=-1.0 / VALUES, scalar2=0.0,
                 op0=ALU.mult, op1=ALU.add,
             )
 
-        def second_moment(u):
-            c, t = divmod(u, PACK)
-            product = work.tile([P, BATCH, PIXELS], BF16)
-            nc.vector.scalar_tensor_tensor(
-                out=product[:], in0=e_passes[c][:, t], scalar=-1.0 / VALUES, in1=xh_units[u][:],
-                op0=ALU.mult, op1=ALU.mult, accum_out=neg_mean_e_xh[:, u : u + 1],
+        def line_of_correction(u):
+            one = slice(u, u + 1)
+            nc.gpsimd.tensor_tensor(out=slope[:, one], in0=sum_cm[:, one], in1=k_slope[:, one], op=ALU.mult)
+            nc.gpsimd.tensor_scalar(
+                out=offset[:, one], in0=sum_cm[:, one], scalar1=k_offset[:, one], scalar2=neg_mean_e[:, one],
+                op0=ALU.mult, op1=ALU.add,
             )
 
         def correction(u):
             c, t = divmod(u, PACK)
+            one = slice(u, u + 1)
             if t == 0:
                 corr_pass = work.tile([P, PACK, BATCH, PIXELS], F32)
                 corr_passes[c] = corr_pass
             nc.scalar.activation(
-                out=corr_passes[c][:, t], in_=xh_units[u][:], func=ACT.Identity,
-                scale=neg_mean_e_xh[:, u : u + 1], bias=neg_mean_e[:, u : u + 1],
+                out=corr_passes[c][:, t], in_=y_units[u][:], func=ACT.Identity,
+                scale=slope[:, one], bias=offset[:, one],
             )
 
         dy_codes = keep.tile([P, PASSES, BATCH, PIXELS], U32, align_bytes=64)
         dy_scales = keep.tile([P, PASSES, BATCH, PIXELS], U8, align_bytes=64)
-        upper = keep.tile([P, BATCH, PX_TILES, C_IN], F32)
+        dy_words = {}
         sums = {}
-        out_view = out.rearrange("b (m p) h w -> b m p (h w)", p=P)
 
-        def quantise_pass(c):
-            dy_words = {}
-            for b in range(BATCH):
-                dy_word = work.tile([P, PIXELS, PACK], BF16, align_bytes=64)
-                nc.vector.tensor_tensor(
-                    out=by_fours_words(dy_word[:]),
-                    in0=by_fours_rows(e_passes[c][:, :, b, :]),
-                    in1=by_fours_rows(corr_passes[c][:, :, b, :]),
-                    op=ALU.add,
-                )
-                dy_words[b] = dy_word
-            for b in range(BATCH):
-                nc.vector.quantize_mx(
-                    out=dy_codes[:, c, b, :].bitcast(E5M2X4),
-                    scales=dy_scales[:, c, b, :],
-                    in_=dy_words[b][:].rearrange("p w t -> p (w t)"),
-                )
-
-        def multiply_pass(c, b, j, start, stop):
-            px = slice(j * P, (j + 1) * P)
-            nc.tensor.matmul_mx(
-                out=sums[(b, j)][:],
-                lhsT=dy_codes[:, c, b, px].bitcast(E5M2X4),
-                lhsT_scale=dy_scales[:, c, b, px],
-                rhs=w_codes[:, c, :].bitcast(E4M3X4),
-                rhs_scale=w_scales[:, c, :],
-                start=start,
-                stop=stop,
+        def add_and_round(c, b):
+            dy_word = work.tile([P, PIXELS, PACK], BF16, align_bytes=64)
+            nc.vector.tensor_tensor(
+                out=by_fours_words(dy_word[:]),
+                in0=by_fours_rows(e_passes[c][:, :, b, :]),
+                in1=by_fours_rows(corr_passes[c][:, :, b, :]),
+                op=ALU.add,
             )
+            dy_words[b] = dy_word
 
-        def finish_pass(c):
-            quantise_pass(c)
-            first = c == 0 or c == UPPER_PASSES
-            last = c == UPPER_PASSES - 1 or c == PASSES - 1
-            for b in range(BATCH):
-                for j in range(PX_TILES):
-                    if first:
-                        acc = psum.tile([P, C_IN], F32, tag="bank")
-                        sums[(b, j)] = acc
-                    multiply_pass(c, b, j, first, last)
-            if c == UPPER_PASSES - 1:
-                for b in range(BATCH):
-                    for j in range(PX_TILES):
-                        nc.scalar.activation(
-                            out=upper[:, b, j, :], in_=sums[(b, j)][:], func=ACT.Copy, scale=att(0, b, j)
-                        )
-            if c == PASSES - 1:
-                for b in range(BATCH):
-                    store_image(b)
+        def quantise_and_multiply(c, b):
+            nc.vector.quantize_mx(
+                out=dy_codes[:, c, b, :].bitcast(E5M2X4),
+                scales=dy_scales[:, c, b, :],
+                in_=dy_words[b][:].rearrange("p w t -> p (w t)"),
+            )
+            opens = c == 0 or c == UPPER_PASSES
+            closes = c == UPPER_PASSES - 1 or c == PASSES - 1
+            for j in range(PX_TILES):
+                px = slice(j * P, (j + 1) * P)
+                if opens:
+                    acc = psum.tile([P, C_IN], F32, tag="bank")
+                    sums[(b, j)] = acc
+                nc.tensor.matmul_mx(
+                    out=sums[(b, j)][:],
+                    lhsT=dy_codes[:, c, b, px].bitcast(E5M2X4),
+                    lhsT_scale=dy_scales[:, c, b, px],
+                    rhs=w_codes[:, c, :].bitcast(E4M3X4),
+                    rhs_scale=w_scales[:, c, :],
+                    start=opens,
+                    stop=closes,
+                )
+
+        upper = keep.tile([P, BATCH, PX_TILES, C_IN], F32)
+
+        def keep_upper(b):
+            for j in range(PX_TILES):
+                nc.scalar.activation(out=upper[:, b, j, :], in_=sums[(b, j)][:], func=ACT.Copy, scale=att(0, b, j))
+
+        out_view = out.rearrange("b (m p) h w -> b m p (h w)", p=P)
 
         def store_image(b):
             by_pixel = []
             for j in range(PX_TILES):
-                total = work.tile([P, C_IN], F32, bufs=2 * PX_TILES)
+                total = work.tile([P, C_IN], F32, bufs=BATCH * PX_TILES)
                 nc.vector.scalar_tensor_tensor(
                     out=total[:], in0=sums[(b, j)][:], scalar=att(1, b, j), in1=upper[:, b, j, :],
                     op0=ALU.mult, op1=ALU.add,
@@ -272,23 +280,39 @@ def tile_gnn_t_v_kernel(
                     nc.tensor.transpose(
                         turned[:, j * P : (j + 1) * P], by_pixel[j][:, m * P : (m + 1) * P], identity[:]
                     )
-                result = work.tile([P, PIXELS], F32, bufs=4)
+                result = work.tile([P, PIXELS], F32, bufs=C_TILES)
                 nc.scalar.copy(out=result[:], in_=turned[:])
                 nc.sync.dma_start(out=out_view[b, m], in_=result[:])
 
-        normalise(0)
-        for i in range(UNITS + 2):
-            if i + 1 < UNITS:
-                normalise(i + 1)
+        for i in range(UNITS + 1):
+            half, due = divmod(i - FIRST_HALF_STEP, STEPS_PER_HALF)
+            due = due == 0 and 0 <= half < UPPER_PASSES * BATCH
+            c_done, b_done = divmod(half, BATCH)
+            if i >= 1:
+                line_of_correction(i - 1)
+            if due:
+                add_and_round(c_done, b_done)
             if i < UNITS:
-                mask_gradient(i)
-            if i >= 2 and (i - 2) % PACK == PACK - 1:
-                finish_pass((i - 2) // PACK)
-            if 1 <= i <= UNITS:
-                second_moment(i - 1)
+                mask_and_sum(i)
+            if due:
+                quantise_and_multiply(c_done, b_done)
             if i < UNITS:
                 scale_gradient(i)
-            if 1 <= i <= UNITS:
+            if i >= 1:
                 correction(i - 1)
-            if i + LOAD_AHEAD < UNITS:
-                load_unit(i + LOAD_AHEAD)
+                if i - 1 + LOAD_AHEAD < UNITS:
+                    load_unit(i - 1 + LOAD_AHEAD)
+            if 0 <= i - WEIGHT_STEP < PASSES:
+                regroup_weights(i - WEIGHT_STEP)
+            if 0 <= i - WEIGHT_STEP - 2 < PASSES:
+                quantise_weights(i - WEIGHT_STEP - 2)
+            if due and c_done == UPPER_PASSES - 1:
+                keep_upper(b_done)
+
+        lower = PASSES - 1
+        for b in range(BATCH):
+            add_and_round(lower, b)
+        for b in range(BATCH):
+            quantise_and_multiply(lower, b)
+        for b in range(BATCH):
+            store_image(b)

@@ -27,7 +27,8 @@ LOAD_AHEAD = 8
 
 FIRST_HALF_STEP = 6
 STEPS_PER_HALF = 2
-WEIGHT_STEP = 3
+HALVES_IN_LOOP = 3
+WEIGHT_STEPS = 3
 
 ROW_GAMMA = 0
 ROW_BETA = ROW_GAMMA + UNITS
@@ -69,15 +70,17 @@ def tile_gnn_t_v_kernel(
         rows = keep.tile([P, P], F32)
         nc.vector.memset(rows_bf16[:], 0.0)
         nc.vector.memset(rows[ROW_F32:P, :], 0.0)
+        addend = keep.tile([P, UNITS, 2], F32)
+        nc.vector.memset(addend[:], 0.0)
         upper_units = UPPER_PASSES * PACK
-        nc.scalar.dma_start(out=rows[ROW_MEAN : ROW_MEAN + UNITS, :], in_=mean.rearrange("(r q) -> r q", q=P))
-        nc.scalar.dma_start(out=rows[ROW_RSTD : ROW_RSTD + UNITS, :], in_=rstd.rearrange("(r q) -> r q", q=P))
+        nc.sync.dma_start(out=rows[ROW_MEAN : ROW_MEAN + UNITS, :], in_=mean.rearrange("(r q) -> r q", q=P))
+        nc.sync.dma_start(out=rows[ROW_RSTD : ROW_RSTD + UNITS, :], in_=rstd.rearrange("(r q) -> r q", q=P))
         for vec_u, vec_l, row in ((gamma_u, gamma_l, ROW_GAMMA), (beta_u, beta_l, ROW_BETA)):
-            nc.scalar.dma_start(out=rows_bf16[row : row + upper_units, :], in_=vec_u.rearrange("(r q) -> r q", q=P))
-            nc.scalar.dma_start(
+            nc.sync.dma_start(out=rows_bf16[row : row + upper_units, :], in_=vec_u.rearrange("(r q) -> r q", q=P))
+            nc.sync.dma_start(
                 out=rows_bf16[row + upper_units : row + UNITS, :], in_=vec_l.rearrange("(r q) -> r q", q=P)
             )
-        nc.scalar.dma_start(
+        nc.sync.dma_start(
             out=rows_bf16[ROW_ATT : ROW_ATT + 2 * BATCH * PX_TILES, :],
             in_=h_att[1:3].rearrange("i b o (j h) w -> (i b o j) (h w)", j=PX_TILES),
         )
@@ -108,8 +111,8 @@ def tile_gnn_t_v_kernel(
 
         for u in range(LOAD_AHEAD):
             load_unit(u)
-            if 0 <= u - (WEIGHT_STEP - 1) < PASSES:
-                load_weights(u - (WEIGHT_STEP - 1))
+            if u % WEIGHT_STEPS == 1:
+                load_weights(u // WEIGHT_STEPS)
 
         nc.vector.tensor_copy(out=rows[0:ROW_F32, :], in_=rows_bf16[:])
         cols_psum = psum.tile([P, C_IN], F32, tag="bank")
@@ -127,21 +130,17 @@ def tile_gnn_t_v_kernel(
 
         z_slope = keep.tile([P, UNITS], F32)
         nc.vector.tensor_tensor(out=z_slope[:], in0=rstd_c, in1=gamma, op=ALU.mult)
-        mean_z_slope = keep.tile([P, UNITS], F32)
-        nc.vector.tensor_tensor(out=mean_z_slope[:], in0=mean_c, in1=z_slope[:], op=ALU.mult)
-        z_thresh = keep.tile([P, UNITS], F32)
-        nc.vector.tensor_tensor(out=z_thresh[:], in0=mean_z_slope[:], in1=beta, op=ALU.subtract)
-        e_scale = keep.tile([P, UNITS], F32)
-        nc.vector.tensor_scalar(out=e_scale[:], in0=z_slope[:], scalar1=0.5, scalar2=None, op0=ALU.mult)
         rstd_sq = keep.tile([P, UNITS], F32)
         nc.vector.tensor_tensor(out=rstd_sq[:], in0=rstd_c, in1=rstd_c, op=ALU.mult)
-        k_slope = keep.tile([P, UNITS], F32)
+        mean_z_slope = keep.tile([P, UNITS], F32)
+        nc.vector.tensor_tensor(out=mean_z_slope[:], in0=mean_c, in1=z_slope[:], op=ALU.mult)
+        e_scale = keep.tile([P, UNITS], F32)
+        nc.vector.tensor_scalar(out=e_scale[:], in0=z_slope[:], scalar1=0.5, scalar2=None, op0=ALU.mult)
+        z_thresh = keep.tile([P, UNITS], F32)
+        nc.vector.tensor_tensor(out=z_thresh[:], in0=mean_z_slope[:], in1=beta, op=ALU.subtract)
+        k_line = keep.tile([P, UNITS, 2], F32)
         nc.vector.scalar_tensor_tensor(
-            out=k_slope[:], in0=rstd_sq[:], scalar=-1.0 / VALUES, in1=e_scale[:], op0=ALU.mult, op1=ALU.mult
-        )
-        k_offset = keep.tile([P, UNITS], F32)
-        nc.vector.scalar_tensor_tensor(
-            out=k_offset[:], in0=k_slope[:], scalar=-1.0, in1=mean_c, op0=ALU.mult, op1=ALU.mult
+            out=k_line[:, :, 0], in0=rstd_sq[:], scalar=-1.0 / VALUES, in1=e_scale[:], op0=ALU.mult, op1=ALU.mult
         )
 
         w_codes = keep.tile([P, PASSES, C_IN], U32, align_bytes=64)
@@ -149,7 +148,7 @@ def tile_gnn_t_v_kernel(
         w_words = {}
 
         def regroup_weights(c):
-            w_word = work.tile([P, C_IN, PACK], BF16, bufs=PASSES, align_bytes=64)
+            w_word = work.tile([P, C_IN, PACK], BF16, align_bytes=64)
             nc.scalar.copy(out=by_fours_words(w_word[:]), in_=by_fours_rows(w_raws[c][:]))
             w_words[c] = w_word
 
@@ -162,26 +161,31 @@ def tile_gnn_t_v_kernel(
 
         sum_cm = keep.tile([P, UNITS], F32)
         sum_e = keep.tile([P, UNITS], F32)
-        neg_mean_e = keep.tile([P, UNITS], F32)
-        slope = keep.tile([P, UNITS], F32)
-        offset = keep.tile([P, UNITS], F32)
+        line = keep.tile([P, UNITS, 2], F32)
+        relu_units = {}
         masked_units = {}
         e_passes = {}
         corr_passes = {}
 
-        def mask_and_sum(u):
+        def find_relu(u):
             one = slice(u, u + 1)
             relu_on = work.tile([P, BATCH, PIXELS], BF16)
             nc.vector.tensor_scalar(
                 out=relu_on[:], in0=y_units[u][:], scalar1=z_slope[:, one], scalar2=z_thresh[:, one],
                 op0=ALU.mult, op1=ALU.is_gt,
             )
+            relu_units[u] = relu_on
+
+        def mask_gradient(u):
             masked = work.tile([P, BATCH, PIXELS], BF16, bufs=3)
-            nc.vector.tensor_tensor(out=masked[:], in0=relu_on[:], in1=g_units[u][:], op=ALU.mult)
+            nc.vector.tensor_tensor(out=masked[:], in0=relu_units[u][:], in1=g_units[u][:], op=ALU.mult)
             masked_units[u] = masked
+
+        def sum_centred(u):
+            one = slice(u, u + 1)
             product = work.tile([P, BATCH, PIXELS], BF16)
             nc.vector.scalar_tensor_tensor(
-                out=product[:], in0=y_units[u][:], scalar=mean_c[:, one], in1=masked[:],
+                out=product[:], in0=y_units[u][:], scalar=mean_c[:, one], in1=masked_units[u][:],
                 op0=ALU.subtract, op1=ALU.mult, accum_out=sum_cm[:, one],
             )
 
@@ -195,28 +199,22 @@ def tile_gnn_t_v_kernel(
                 out=e_passes[c][:, t], in_=masked_units[u][:], func=ACT.Copy,
                 scale=e_scale[:, one], accum_out=sum_e[:, one],
             )
-            nc.gpsimd.tensor_scalar(
-                out=neg_mean_e[:, one], in0=sum_e[:, one], scalar1=-1.0 / VALUES, scalar2=0.0,
-                op0=ALU.mult, op1=ALU.add,
-            )
+            nc.scalar.activation(out=addend[:, u, 1:2], in_=sum_e[:, one], func=ACT.Copy, scale=-1.0 / VALUES)
 
         def line_of_correction(u):
-            one = slice(u, u + 1)
-            nc.gpsimd.tensor_tensor(out=slope[:, one], in0=sum_cm[:, one], in1=k_slope[:, one], op=ALU.mult)
-            nc.gpsimd.tensor_scalar(
-                out=offset[:, one], in0=sum_cm[:, one], scalar1=k_offset[:, one], scalar2=neg_mean_e[:, one],
+            nc.vector.scalar_tensor_tensor(
+                out=line[:, u, :], in0=k_line[:, u, :], scalar=sum_cm[:, u : u + 1], in1=addend[:, u, :],
                 op0=ALU.mult, op1=ALU.add,
             )
 
         def correction(u):
             c, t = divmod(u, PACK)
-            one = slice(u, u + 1)
             if t == 0:
                 corr_pass = work.tile([P, PACK, BATCH, PIXELS], F32)
                 corr_passes[c] = corr_pass
             nc.scalar.activation(
                 out=corr_passes[c][:, t], in_=y_units[u][:], func=ACT.Identity,
-                scale=slope[:, one], bias=offset[:, one],
+                scale=line[:, u, 0:1], bias=line[:, u, 1:2],
             )
 
         dy_codes = keep.tile([P, PASSES, BATCH, PIXELS], U32, align_bytes=64)
@@ -232,13 +230,13 @@ def tile_gnn_t_v_kernel(
                 in1=by_fours_rows(corr_passes[c][:, :, b, :]),
                 op=ALU.add,
             )
-            dy_words[b] = dy_word
+            dy_words[(c, b)] = dy_word
 
         def quantise_and_multiply(c, b):
             nc.vector.quantize_mx(
                 out=dy_codes[:, c, b, :].bitcast(E5M2X4),
                 scales=dy_scales[:, c, b, :],
-                in_=dy_words[b][:].rearrange("p w t -> p (w t)"),
+                in_=dy_words[(c, b)][:].rearrange("p w t -> p (w t)"),
             )
             opens = c == 0 or c == UPPER_PASSES
             closes = c == UPPER_PASSES - 1 or c == PASSES - 1
@@ -263,56 +261,62 @@ def tile_gnn_t_v_kernel(
             for j in range(PX_TILES):
                 nc.scalar.activation(out=upper[:, b, j, :], in_=sums[(b, j)][:], func=ACT.Copy, scale=att(0, b, j))
 
-        out_view = out.rearrange("b (m p) h w -> b m p (h w)", p=P)
+        out_view = out.rearrange("b (m p) (j h) w -> b j p m (h w)", p=P, j=PX_TILES)
 
-        def store_image(b):
-            by_pixel = []
-            for j in range(PX_TILES):
-                total = work.tile([P, C_IN], F32, bufs=BATCH * PX_TILES)
-                nc.vector.scalar_tensor_tensor(
-                    out=total[:], in0=sums[(b, j)][:], scalar=att(1, b, j), in1=upper[:, b, j, :],
-                    op0=ALU.mult, op1=ALU.add,
-                )
-                by_pixel.append(total)
+        def store_pixels(b, j):
+            total = work.tile([P, C_IN], F32, bufs=4)
+            nc.vector.scalar_tensor_tensor(
+                out=total[:], in0=sums[(b, j)][:], scalar=att(1, b, j), in1=upper[:, b, j, :],
+                op0=ALU.mult, op1=ALU.add,
+            )
+            turned = psum.tile([P, C_TILES, P], F32, tag="bank")
             for m in range(C_TILES):
-                turned = psum.tile([P, PIXELS], F32, tag="bank")
-                for j in range(PX_TILES):
-                    nc.tensor.transpose(
-                        turned[:, j * P : (j + 1) * P], by_pixel[j][:, m * P : (m + 1) * P], identity[:]
-                    )
-                result = work.tile([P, PIXELS], F32, bufs=C_TILES)
-                nc.scalar.copy(out=result[:], in_=turned[:])
-                nc.sync.dma_start(out=out_view[b, m], in_=result[:])
+                nc.tensor.transpose(turned[:, m, :], total[:, m * P : (m + 1) * P], identity[:])
+            result = work.tile([P, C_TILES, P], F32, bufs=4)
+            nc.scalar.copy(out=result[:], in_=turned[:])
+            nc.sync.dma_start(out=out_view[b, j], in_=result[:])
 
+        find_relu(0)
+        nc.vector.scalar_tensor_tensor(
+            out=k_line[:, :, 1], in0=k_line[:, :, 0], scalar=-1.0, in1=mean_c, op0=ALU.mult, op1=ALU.mult
+        )
         for i in range(UNITS + 1):
-            half, due = divmod(i - FIRST_HALF_STEP, STEPS_PER_HALF)
-            due = due == 0 and 0 <= half < UPPER_PASSES * BATCH
+            half, odd_step = divmod(i - FIRST_HALF_STEP, STEPS_PER_HALF)
+            finishing = odd_step == 0 and 0 <= half < HALVES_IN_LOOP
             c_done, b_done = divmod(half, BATCH)
-            if i >= 1:
-                line_of_correction(i - 1)
-            if due:
+            if finishing:
                 add_and_round(c_done, b_done)
             if i < UNITS:
-                mask_and_sum(i)
-            if due:
+                mask_gradient(i)
+            if i >= 1:
+                line_of_correction(i - 1)
+            if i + 1 < UNITS:
+                find_relu(i + 1)
+            if i < UNITS:
+                sum_centred(i)
+            if finishing:
                 quantise_and_multiply(c_done, b_done)
+            if i % WEIGHT_STEPS == 1 and 0 <= i // WEIGHT_STEPS - 1 < PASSES:
+                quantise_weights(i // WEIGHT_STEPS - 1)
             if i < UNITS:
                 scale_gradient(i)
             if i >= 1:
                 correction(i - 1)
                 if i - 1 + LOAD_AHEAD < UNITS:
                     load_unit(i - 1 + LOAD_AHEAD)
-            if 0 <= i - WEIGHT_STEP < PASSES:
-                regroup_weights(i - WEIGHT_STEP)
-            if 0 <= i - WEIGHT_STEP - 2 < PASSES:
-                quantise_weights(i - WEIGHT_STEP - 2)
-            if due and c_done == UPPER_PASSES - 1:
+            if i % WEIGHT_STEPS == 2 and i // WEIGHT_STEPS < PASSES:
+                regroup_weights(i // WEIGHT_STEPS)
+            if finishing and c_done == UPPER_PASSES - 1:
                 keep_upper(b_done)
 
         lower = PASSES - 1
-        for b in range(BATCH):
-            add_and_round(lower, b)
+        add_and_round(UPPER_PASSES - 1, 1)
+        add_and_round(lower, 0)
+        quantise_and_multiply(UPPER_PASSES - 1, 1)
+        keep_upper(1)
+        add_and_round(lower, 1)
         for b in range(BATCH):
             quantise_and_multiply(lower, b)
         for b in range(BATCH):
-            store_image(b)
+            for j in range(PX_TILES):
+                store_pixels(b, j)

@@ -28,7 +28,11 @@ LOAD_AHEAD = 8
 FIRST_HALF_STEP = 6
 STEPS_PER_HALF = 2
 HALVES_IN_LOOP = 3
-WEIGHT_STEPS = 3
+VECTOR_COPIES = 2
+WEIGHT_EVERY = 2
+WEIGHT_LOAD_UNIT = 3
+WEIGHT_REGROUP_STEP = 4
+WEIGHT_QUANTISE_STEP = 6
 
 ROW_GAMMA = 0
 ROW_BETA = ROW_GAMMA + UNITS
@@ -55,6 +59,11 @@ def by_fours_words(ap):
     return ap.rearrange("p (c i) t -> p c t i", i=PACK)
 
 
+def weight_pass_at(distance):
+    c, rest = divmod(distance, WEIGHT_EVERY)
+    return c if rest == 0 and 0 <= c < PASSES else None
+
+
 def tile_gnn_t_v_kernel(
     tc, p_nodes, h_nodes, f_nodes, xp, h_att, Wu, Wl, gamma_u, beta_u, gamma_l, beta_l, y, mean, rstd, grad_out, out
 ):
@@ -68,10 +77,10 @@ def tile_gnn_t_v_kernel(
 
         rows_bf16 = keep.tile([ROW_F32, P], BF16)
         rows = keep.tile([P, P], F32)
-        nc.vector.memset(rows_bf16[:], 0.0)
-        nc.vector.memset(rows[ROW_F32:P, :], 0.0)
+        nc.gpsimd.memset(rows_bf16[:], 0.0)
+        nc.gpsimd.memset(rows[ROW_F32:P, :], 0.0)
         addend = keep.tile([P, UNITS, 2], F32)
-        nc.vector.memset(addend[:], 0.0)
+        nc.gpsimd.memset(addend[:], 0.0)
         upper_units = UPPER_PASSES * PACK
         nc.sync.dma_start(out=rows[ROW_MEAN : ROW_MEAN + UNITS, :], in_=mean.rearrange("(r q) -> r q", q=P))
         nc.sync.dma_start(out=rows[ROW_RSTD : ROW_RSTD + UNITS, :], in_=rstd.rearrange("(r q) -> r q", q=P))
@@ -111,8 +120,8 @@ def tile_gnn_t_v_kernel(
 
         for u in range(LOAD_AHEAD):
             load_unit(u)
-            if u % WEIGHT_STEPS == 1:
-                load_weights(u // WEIGHT_STEPS)
+            if weight_pass_at(u - WEIGHT_LOAD_UNIT) is not None:
+                load_weights(weight_pass_at(u - WEIGHT_LOAD_UNIT))
 
         nc.vector.tensor_copy(out=rows[0:ROW_F32, :], in_=rows_bf16[:])
         cols_psum = psum.tile([P, C_IN], F32, tag="bank")
@@ -263,7 +272,7 @@ def tile_gnn_t_v_kernel(
 
         out_view = out.rearrange("b (m p) (j h) w -> b j p m (h w)", p=P, j=PX_TILES)
 
-        def store_pixels(b, j):
+        def combine_and_turn(b, j):
             total = work.tile([P, C_IN], F32, bufs=4)
             nc.vector.scalar_tensor_tensor(
                 out=total[:], in0=sums[(b, j)][:], scalar=att(1, b, j), in1=upper[:, b, j, :],
@@ -272,8 +281,14 @@ def tile_gnn_t_v_kernel(
             turned = psum.tile([P, C_TILES, P], F32, tag="bank")
             for m in range(C_TILES):
                 nc.tensor.transpose(turned[:, m, :], total[:, m * P : (m + 1) * P], identity[:])
+            return turned
+
+        def store_pixels(b, j, turned, by_vector):
             result = work.tile([P, C_TILES, P], F32, bufs=4)
-            nc.scalar.copy(out=result[:], in_=turned[:])
+            if by_vector:
+                nc.vector.tensor_copy(out=result[:], in_=turned[:])
+            else:
+                nc.scalar.copy(out=result[:], in_=turned[:])
             nc.sync.dma_start(out=out_view[b, j], in_=result[:])
 
         find_relu(0)
@@ -294,22 +309,21 @@ def tile_gnn_t_v_kernel(
                 find_relu(i + 1)
             if i < UNITS:
                 sum_centred(i)
+            if weight_pass_at(i - WEIGHT_QUANTISE_STEP) is not None:
+                quantise_weights(weight_pass_at(i - WEIGHT_QUANTISE_STEP))
             if finishing:
                 quantise_and_multiply(c_done, b_done)
-            if i % WEIGHT_STEPS == 1 and 0 <= i // WEIGHT_STEPS - 1 < PASSES:
-                quantise_weights(i // WEIGHT_STEPS - 1)
             if i < UNITS:
                 scale_gradient(i)
             if i >= 1:
                 correction(i - 1)
                 if i - 1 + LOAD_AHEAD < UNITS:
                     load_unit(i - 1 + LOAD_AHEAD)
-            if i % WEIGHT_STEPS == 2 and i // WEIGHT_STEPS < PASSES:
-                regroup_weights(i // WEIGHT_STEPS)
-            if finishing and c_done == UPPER_PASSES - 1:
-                keep_upper(b_done)
+            if weight_pass_at(i - WEIGHT_REGROUP_STEP) is not None:
+                regroup_weights(weight_pass_at(i - WEIGHT_REGROUP_STEP))
 
         lower = PASSES - 1
+        keep_upper(0)
         add_and_round(UPPER_PASSES - 1, 1)
         add_and_round(lower, 0)
         quantise_and_multiply(UPPER_PASSES - 1, 1)
@@ -317,6 +331,13 @@ def tile_gnn_t_v_kernel(
         add_and_round(lower, 1)
         for b in range(BATCH):
             quantise_and_multiply(lower, b)
-        for b in range(BATCH):
-            for j in range(PX_TILES):
-                store_pixels(b, j)
+        tiles = [(b, j) for b in range(BATCH) for j in range(PX_TILES)]
+        last_turned = {}
+        for b, j in tiles:
+            turned = combine_and_turn(b, j)
+            if (b, j) in tiles[-VECTOR_COPIES:]:
+                last_turned[(b, j)] = turned
+            else:
+                store_pixels(b, j, turned, False)
+        for b, j in tiles[-VECTOR_COPIES:]:
+            store_pixels(b, j, last_turned[(b, j)], True)

@@ -33,6 +33,8 @@ WEIGHT_EVERY = 2
 WEIGHT_LOAD_UNIT = 3
 WEIGHT_REGROUP_STEP = 4
 WEIGHT_QUANTISE_STEP = 6
+ATTENTION_STEP = 3
+LATER_PASSES = (1, 2)
 
 ROW_GAMMA = 0
 ROW_BETA = ROW_GAMMA + UNITS
@@ -75,27 +77,14 @@ def tile_gnn_t_v_kernel(
         psum = ctx.enter_context(tc.psum_pool(name="psum", bufs=8))
         ctx.enter_context(tc.manual_schedule())
 
-        rows_bf16 = keep.tile([ROW_F32, P], BF16)
-        rows = keep.tile([P, P], F32)
+        rows_f32 = keep.tile([P, P], F32)
+        rows_bf16 = keep.tile([P, P], BF16)
+        att_rows = keep.tile([P, P], BF16)
+        nc.gpsimd.memset(rows_f32[:], 0.0)
         nc.gpsimd.memset(rows_bf16[:], 0.0)
-        nc.gpsimd.memset(rows[ROW_F32:P, :], 0.0)
         addend = keep.tile([P, UNITS, 2], F32)
         nc.gpsimd.memset(addend[:], 0.0)
         upper_units = UPPER_PASSES * PACK
-        nc.sync.dma_start(out=rows[ROW_MEAN : ROW_MEAN + UNITS, :], in_=mean.rearrange("(r q) -> r q", q=P))
-        nc.sync.dma_start(out=rows[ROW_RSTD : ROW_RSTD + UNITS, :], in_=rstd.rearrange("(r q) -> r q", q=P))
-        for vec_u, vec_l, row in ((gamma_u, gamma_l, ROW_GAMMA), (beta_u, beta_l, ROW_BETA)):
-            nc.sync.dma_start(out=rows_bf16[row : row + upper_units, :], in_=vec_u.rearrange("(r q) -> r q", q=P))
-            nc.sync.dma_start(
-                out=rows_bf16[row + upper_units : row + UNITS, :], in_=vec_l.rearrange("(r q) -> r q", q=P)
-            )
-        nc.sync.dma_start(
-            out=rows_bf16[ROW_ATT : ROW_ATT + 2 * BATCH * PX_TILES, :],
-            in_=h_att[1:3].rearrange("i b o (j h) w -> (i b o j) (h w)", j=PX_TILES),
-        )
-        identity = keep.tile([P, P], F32)
-        make_identity(nc, identity[:])
-
         w_views = [Wu.rearrange("(c t p) n -> c p t n", t=PACK, p=P)[c] for c in range(UPPER_PASSES)]
         w_views.append(Wl.rearrange("(t p) n -> p t n", p=P))
         w_raws = {}
@@ -104,6 +93,20 @@ def tile_gnn_t_v_kernel(
             w_raw = keep.tile([P, PACK, C_IN], BF16, name="w_raw%d" % c)
             nc.sync.dma_start(out=w_raw[:], in_=w_views[c])
             w_raws[c] = w_raw
+
+        load_weights(0)
+        nc.sync.dma_start(out=rows_f32[0:UNITS, :], in_=mean.rearrange("(r q) -> r q", q=P))
+        nc.sync.dma_start(out=rows_f32[UNITS : 2 * UNITS, :], in_=rstd.rearrange("(r q) -> r q", q=P))
+        for vec_u, vec_l, row in ((gamma_u, gamma_l, 0), (beta_u, beta_l, UNITS)):
+            nc.sync.dma_start(out=rows_bf16[row : row + upper_units, :], in_=vec_u.rearrange("(r q) -> r q", q=P))
+            nc.sync.dma_start(
+                out=rows_bf16[row + upper_units : row + UNITS, :], in_=vec_l.rearrange("(r q) -> r q", q=P)
+            )
+        identity = keep.tile([P, P], F32)
+        make_identity(nc, identity[:])
+        identity_bf16 = keep.tile([P, P], BF16)
+        make_identity(nc, identity_bf16[:])
+        nc.gpsimd.memset(att_rows[:], 0.0)
 
         y_view = y.rearrange("b (u p) h w -> u p b (h w)", p=P)
         g_view = grad_out.rearrange("n b (v p) h w -> n v p b (h w)", p=P)
@@ -120,27 +123,63 @@ def tile_gnn_t_v_kernel(
 
         for u in range(LOAD_AHEAD):
             load_unit(u)
-            if weight_pass_at(u - WEIGHT_LOAD_UNIT) is not None:
+            if u == 1:
+                nc.sync.dma_start(
+                    out=att_rows[0 : 2 * BATCH * PX_TILES, :],
+                    in_=h_att[1:3].rearrange("i b o (j h) w -> (i b o j) (h w)", j=PX_TILES),
+                )
+            if weight_pass_at(u - WEIGHT_LOAD_UNIT) in LATER_PASSES:
                 load_weights(weight_pass_at(u - WEIGHT_LOAD_UNIT))
 
-        nc.vector.tensor_copy(out=rows[0:ROW_F32, :], in_=rows_bf16[:])
-        cols_psum = psum.tile([P, C_IN], F32, tag="bank")
-        nc.tensor.transpose(cols_psum[:, 0:P], rows[:], identity[:])
-        cols = keep.tile([P, P], F32)
-        nc.vector.tensor_copy(out=cols[:], in_=cols_psum[:, 0:P])
-        gamma = cols[:, ROW_GAMMA : ROW_GAMMA + UNITS]
-        beta = cols[:, ROW_BETA : ROW_BETA + UNITS]
-        mean_c = cols[:, ROW_MEAN : ROW_MEAN + UNITS]
-        rstd_c = cols[:, ROW_RSTD : ROW_RSTD + UNITS]
+        w_codes = keep.tile([P, PASSES, C_IN], U32, align_bytes=64)
+        w_scales = keep.tile([P, PASSES, C_IN], U8, align_bytes=64)
+        w_words = {}
+
+        def regroup_weights(c, by_vector=False):
+            w_word = work.tile([P, C_IN, PACK], BF16, align_bytes=64)
+            if by_vector:
+                nc.vector.tensor_copy(out=by_fours_words(w_word[:]), in_=by_fours_rows(w_raws[c][:]))
+            else:
+                nc.scalar.copy(out=by_fours_words(w_word[:]), in_=by_fours_rows(w_raws[c][:]))
+            w_words[c] = w_word
+
+        def quantise_weights(c):
+            nc.vector.quantize_mx(
+                out=w_codes[:, c, :].bitcast(E4M3X4),
+                scales=w_scales[:, c, :],
+                in_=w_words[c][:].rearrange("p n t -> p (n t)"),
+            )
+
+        regroup_weights(0, True)
+        quantise_weights(0)
+
+        f32_psum = psum.tile([P, C_IN], F32, tag="bank")
+        nc.tensor.transpose(f32_psum[:, 0:P], rows_f32[:], identity[:])
+        bf16_psum = psum.tile([P, 2 * C_IN], BF16, tag="bank")
+        nc.tensor.transpose(bf16_psum[:, 0:P], rows_bf16[:], identity_bf16[:])
+        cols_f32 = keep.tile([P, 2 * UNITS], F32)
+        nc.vector.tensor_copy(out=cols_f32[:], in_=f32_psum[:, 0 : 2 * UNITS])
+        mean_c = cols_f32[:, 0:UNITS]
+        rstd_c = cols_f32[:, UNITS : 2 * UNITS]
+        rstd_sq = keep.tile([P, UNITS], F32)
+        nc.vector.tensor_tensor(out=rstd_sq[:], in0=rstd_c, in1=rstd_c, op=ALU.mult)
+        cols_bf16 = keep.tile([P, 2 * UNITS], F32)
+        nc.vector.tensor_copy(out=cols_bf16[:], in_=bf16_psum[:, 0 : 2 * UNITS])
+        gamma = cols_bf16[:, 0:UNITS]
+        beta = cols_bf16[:, UNITS : 2 * UNITS]
+        att_cols = keep.tile([P, 2 * BATCH * PX_TILES], F32)
+
+        def turn_attention():
+            att_psum = psum.tile([P, 2 * C_IN], BF16, tag="bank")
+            nc.tensor.transpose(att_psum[:, 0:P], att_rows[:], identity_bf16[:])
+            nc.scalar.copy(out=att_cols[:], in_=att_psum[:, 0 : 2 * BATCH * PX_TILES])
 
         def att(i, b, j):
-            r = ROW_ATT + (i * BATCH + b) * PX_TILES + j
-            return cols[:, r : r + 1]
+            r = (i * BATCH + b) * PX_TILES + j
+            return att_cols[:, r : r + 1]
 
         z_slope = keep.tile([P, UNITS], F32)
         nc.vector.tensor_tensor(out=z_slope[:], in0=rstd_c, in1=gamma, op=ALU.mult)
-        rstd_sq = keep.tile([P, UNITS], F32)
-        nc.vector.tensor_tensor(out=rstd_sq[:], in0=rstd_c, in1=rstd_c, op=ALU.mult)
         mean_z_slope = keep.tile([P, UNITS], F32)
         nc.vector.tensor_tensor(out=mean_z_slope[:], in0=mean_c, in1=z_slope[:], op=ALU.mult)
         e_scale = keep.tile([P, UNITS], F32)
@@ -151,22 +190,6 @@ def tile_gnn_t_v_kernel(
         nc.vector.scalar_tensor_tensor(
             out=k_line[:, :, 0], in0=rstd_sq[:], scalar=-1.0 / VALUES, in1=e_scale[:], op0=ALU.mult, op1=ALU.mult
         )
-
-        w_codes = keep.tile([P, PASSES, C_IN], U32, align_bytes=64)
-        w_scales = keep.tile([P, PASSES, C_IN], U8, align_bytes=64)
-        w_words = {}
-
-        def regroup_weights(c):
-            w_word = work.tile([P, C_IN, PACK], BF16, align_bytes=64)
-            nc.scalar.copy(out=by_fours_words(w_word[:]), in_=by_fours_rows(w_raws[c][:]))
-            w_words[c] = w_word
-
-        def quantise_weights(c):
-            nc.vector.quantize_mx(
-                out=w_codes[:, c, :].bitcast(E4M3X4),
-                scales=w_scales[:, c, :],
-                in_=w_words[c][:].rearrange("p n t -> p (n t)"),
-            )
 
         sum_cm = keep.tile([P, UNITS], F32)
         sum_e = keep.tile([P, UNITS], F32)
@@ -309,7 +332,7 @@ def tile_gnn_t_v_kernel(
                 find_relu(i + 1)
             if i < UNITS:
                 sum_centred(i)
-            if weight_pass_at(i - WEIGHT_QUANTISE_STEP) is not None:
+            if weight_pass_at(i - WEIGHT_QUANTISE_STEP) in LATER_PASSES:
                 quantise_weights(weight_pass_at(i - WEIGHT_QUANTISE_STEP))
             if finishing:
                 quantise_and_multiply(c_done, b_done)
@@ -319,8 +342,10 @@ def tile_gnn_t_v_kernel(
                 correction(i - 1)
                 if i - 1 + LOAD_AHEAD < UNITS:
                     load_unit(i - 1 + LOAD_AHEAD)
-            if weight_pass_at(i - WEIGHT_REGROUP_STEP) is not None:
+            if weight_pass_at(i - WEIGHT_REGROUP_STEP) in LATER_PASSES:
                 regroup_weights(weight_pass_at(i - WEIGHT_REGROUP_STEP))
+            if i == ATTENTION_STEP:
+                turn_attention()
 
         lower = PASSES - 1
         keep_upper(0)

@@ -307,7 +307,7 @@ def tile_gnn_t_v_kernel(
             return turned
 
         def store_pixels(b, j, turned, by_vector):
-            result = work.tile([P, C_TILES, P], F32, bufs=4)
+            result = work.tile([P, C_TILES, P], F32, bufs=len(tiles))
             if by_vector:
                 nc.vector.tensor_copy(out=result[:], in_=turned[:])
             else:

@@ -306,6 +306,23 @@ def tile_gnn_t_v_kernel(
                 nc.tensor.transpose(turned[:, m, :], total[:, m * P : (m + 1) * P], identity[:])
             return turned
 
+        def scale_lower(b, j):
+            low = work.tile([P, C_IN], F32, bufs=4)
+            nc.scalar.activation(out=low[:], in_=sums[(b, j)][:], func=ACT.Copy, scale=att(1, b, j))
+            return low
+
+        def turn_and_add(b, j, low):
+            turned = psum.tile([P, C_TILES, P], F32, tag="bank")
+            for m in range(C_TILES):
+                cols = slice(m * P, (m + 1) * P)
+                nc.tensor.matmul(
+                    turned[:, m, :], lhsT=upper[:, b, j, cols], rhs=identity[:], is_transpose=True, start=True, stop=False
+                )
+                nc.tensor.matmul(
+                    turned[:, m, :], lhsT=low[:, cols], rhs=identity[:], is_transpose=True, start=False, stop=True
+                )
+            return turned
+
         def store_pixels(b, j, turned, by_vector):
             result = work.tile([P, C_TILES, P], F32, bufs=len(tiles))
             if by_vector:
@@ -348,21 +365,19 @@ def tile_gnn_t_v_kernel(
                 turn_attention()
 
         lower = PASSES - 1
+        tiles = [(b, j) for b in range(BATCH) for j in range(PX_TILES)]
         keep_upper(0)
         add_and_round(UPPER_PASSES - 1, 1)
         add_and_round(lower, 0)
         quantise_and_multiply(UPPER_PASSES - 1, 1)
+        quantise_and_multiply(lower, 0)
         keep_upper(1)
         add_and_round(lower, 1)
-        for b in range(BATCH):
-            quantise_and_multiply(lower, b)
-        tiles = [(b, j) for b in range(BATCH) for j in range(PX_TILES)]
-        last_turned = {}
-        for b, j in tiles:
-            turned = combine_and_turn(b, j)
-            if (b, j) in tiles[-VECTOR_COPIES:]:
-                last_turned[(b, j)] = turned
-            else:
-                store_pixels(b, j, turned, False)
-        for b, j in tiles[-VECTOR_COPIES:]:
-            store_pixels(b, j, last_turned[(b, j)], True)
+        lows = [scale_lower(0, j) for j in range(PX_TILES)]
+        turned_0 = [turn_and_add(0, j, lows[j]) for j in range(PX_TILES)]
+        quantise_and_multiply(lower, 1)
+        for j in range(PX_TILES):
+            store_pixels(0, j, turned_0[j], False)
+        turned_1 = [combine_and_turn(1, j) for j in range(PX_TILES)]
+        for j in range(PX_TILES):
+            store_pixels(1, j, turned_1[j], j % 2 == 1)

@@ -74,7 +74,7 @@ def tile_gnn_t_v_kernel(
         keep = ctx.enter_context(tc.tile_pool(name="keep", bufs=1))
         loads = ctx.enter_context(tc.tile_pool(name="loads", bufs=LOAD_AHEAD))
         work = ctx.enter_context(tc.tile_pool(name="work", bufs=2))
-        psum = ctx.enter_context(tc.psum_pool(name="psum", bufs=8))
+        psum = ctx.enter_context(tc.psum_pool(name="psum", bufs=4))
         ctx.enter_context(tc.manual_schedule())
 
         rows_f32 = keep.tile([P, P], F32)
@@ -153,9 +153,9 @@ def tile_gnn_t_v_kernel(
         regroup_weights(0, True)
         quantise_weights(0)
 
-        f32_psum = psum.tile([P, C_IN], F32, tag="bank")
+        f32_psum = psum.tile([P, C_IN], F32, tag="b")
         nc.tensor.transpose(f32_psum[:, 0:P], rows_f32[:], identity[:])
-        bf16_psum = psum.tile([P, 2 * C_IN], BF16, tag="bank")
+        bf16_psum = psum.tile([P, 2 * C_IN], BF16, tag="b")
         nc.tensor.transpose(bf16_psum[:, 0:P], rows_bf16[:], identity_bf16[:])
         cols_f32 = keep.tile([P, 2 * UNITS], F32)
         nc.vector.tensor_copy(out=cols_f32[:], in_=f32_psum[:, 0 : 2 * UNITS])
@@ -163,14 +163,12 @@ def tile_gnn_t_v_kernel(
         rstd_c = cols_f32[:, UNITS : 2 * UNITS]
         rstd_sq = keep.tile([P, UNITS], F32)
         nc.vector.tensor_tensor(out=rstd_sq[:], in0=rstd_c, in1=rstd_c, op=ALU.mult)
-        cols_bf16 = keep.tile([P, 2 * UNITS], F32)
-        nc.vector.tensor_copy(out=cols_bf16[:], in_=bf16_psum[:, 0 : 2 * UNITS])
-        gamma = cols_bf16[:, 0:UNITS]
-        beta = cols_bf16[:, UNITS : 2 * UNITS]
+        gamma = bf16_psum[:, 0:UNITS]
+        beta = bf16_psum[:, UNITS : 2 * UNITS]
         att_cols = keep.tile([P, 2 * BATCH * PX_TILES], F32)
 
         def turn_attention():
-            att_psum = psum.tile([P, 2 * C_IN], BF16, tag="bank")
+            att_psum = psum.tile([P, 2 * C_IN], BF16, tag="b")
             nc.tensor.transpose(att_psum[:, 0:P], att_rows[:], identity_bf16[:])
             nc.scalar.copy(out=att_cols[:], in_=att_psum[:, 0 : 2 * BATCH * PX_TILES])
 
@@ -187,9 +185,6 @@ def tile_gnn_t_v_kernel(
         z_thresh = keep.tile([P, UNITS], F32)
         nc.vector.tensor_tensor(out=z_thresh[:], in0=mean_z_slope[:], in1=beta, op=ALU.subtract)
         k_line = keep.tile([P, UNITS, 2], F32)
-        nc.vector.scalar_tensor_tensor(
-            out=k_line[:, :, 0], in0=rstd_sq[:], scalar=-1.0 / VALUES, in1=e_scale[:], op0=ALU.mult, op1=ALU.mult
-        )
 
         sum_cm = keep.tile([P, UNITS], F32)
         sum_e = keep.tile([P, UNITS], F32)
@@ -264,28 +259,34 @@ def tile_gnn_t_v_kernel(
             )
             dy_words[(c, b)] = dy_word
 
-        def quantise_and_multiply(c, b):
+        def quantise(c, b):
             nc.vector.quantize_mx(
                 out=dy_codes[:, c, b, :].bitcast(E5M2X4),
                 scales=dy_scales[:, c, b, :],
                 in_=dy_words[(c, b)][:].rearrange("p w t -> p (w t)"),
             )
+
+        def multiply(c, b, j):
             opens = c == 0 or c == UPPER_PASSES
             closes = c == UPPER_PASSES - 1 or c == PASSES - 1
+            px = slice(j * P, (j + 1) * P)
+            if opens:
+                acc = psum.tile([P, C_IN], F32, tag="a" if (c == 0 and b == 0) else "b")
+                sums[(b, j)] = acc
+            nc.tensor.matmul_mx(
+                out=sums[(b, j)][:],
+                lhsT=dy_codes[:, c, b, px].bitcast(E5M2X4),
+                lhsT_scale=dy_scales[:, c, b, px],
+                rhs=w_codes[:, c, :].bitcast(E4M3X4),
+                rhs_scale=w_scales[:, c, :],
+                start=opens,
+                stop=closes,
+            )
+
+        def quantise_and_multiply(c, b):
+            quantise(c, b)
             for j in range(PX_TILES):
-                px = slice(j * P, (j + 1) * P)
-                if opens:
-                    acc = psum.tile([P, C_IN], F32, tag="bank")
-                    sums[(b, j)] = acc
-                nc.tensor.matmul_mx(
-                    out=sums[(b, j)][:],
-                    lhsT=dy_codes[:, c, b, px].bitcast(E5M2X4),
-                    lhsT_scale=dy_scales[:, c, b, px],
-                    rhs=w_codes[:, c, :].bitcast(E4M3X4),
-                    rhs_scale=w_scales[:, c, :],
-                    start=opens,
-                    stop=closes,
-                )
+                multiply(c, b, j)
 
         upper = keep.tile([P, BATCH, PX_TILES, C_IN], F32)
 
@@ -301,7 +302,7 @@ def tile_gnn_t_v_kernel(
                 out=total[:], in0=sums[(b, j)][:], scalar=att(1, b, j), in1=upper[:, b, j, :],
                 op0=ALU.mult, op1=ALU.add,
             )
-            turned = psum.tile([P, C_TILES, P], F32, tag="bank")
+            turned = psum.tile([P, C_TILES, P], F32, tag="b")
             for m in range(C_TILES):
                 nc.tensor.transpose(turned[:, m, :], total[:, m * P : (m + 1) * P], identity[:])
             return turned
@@ -311,17 +312,12 @@ def tile_gnn_t_v_kernel(
             nc.scalar.activation(out=low[:], in_=sums[(b, j)][:], func=ACT.Copy, scale=att(1, b, j))
             return low
 
-        def turn_and_add(b, j, low):
-            turned = psum.tile([P, C_TILES, P], F32, tag="bank")
+        def turn_into(turned, source, first):
             for m in range(C_TILES):
-                cols = slice(m * P, (m + 1) * P)
                 nc.tensor.matmul(
-                    turned[:, m, :], lhsT=upper[:, b, j, cols], rhs=identity[:], is_transpose=True, start=True, stop=False
+                    turned[:, m, :], lhsT=source[:, m * P : (m + 1) * P], rhs=identity[:], is_transpose=True,
+                    start=first and m == 0, stop=(not first) and m == C_TILES - 1,
                 )
-                nc.tensor.matmul(
-                    turned[:, m, :], lhsT=low[:, cols], rhs=identity[:], is_transpose=True, start=False, stop=True
-                )
-            return turned
 
         def store_pixels(b, j, turned, by_vector):
             result = work.tile([P, C_TILES, P], F32, bufs=len(tiles))
@@ -332,6 +328,9 @@ def tile_gnn_t_v_kernel(
             nc.sync.dma_start(out=out_view[b, j], in_=result[:])
 
         find_relu(0)
+        nc.vector.scalar_tensor_tensor(
+            out=k_line[:, :, 0], in0=rstd_sq[:], scalar=-1.0 / VALUES, in1=e_scale[:], op0=ALU.mult, op1=ALU.mult
+        )
         nc.vector.scalar_tensor_tensor(
             out=k_line[:, :, 1], in0=k_line[:, :, 0], scalar=-1.0, in1=mean_c, op0=ALU.mult, op1=ALU.mult
         )
@@ -367,17 +366,29 @@ def tile_gnn_t_v_kernel(
         lower = PASSES - 1
         tiles = [(b, j) for b in range(BATCH) for j in range(PX_TILES)]
         keep_upper(0)
+        turned_0 = []
+        for j in range(PX_TILES):
+            turned = psum.tile([P, C_TILES, P], F32, tag="a")
+            turn_into(turned, upper[:, 0, j, :], True)
+            turned_0.append(turned)
         add_and_round(UPPER_PASSES - 1, 1)
         add_and_round(lower, 0)
         quantise_and_multiply(UPPER_PASSES - 1, 1)
-        quantise_and_multiply(lower, 0)
+        quantise(lower, 0)
         keep_upper(1)
+        for j in range(PX_TILES):
+            multiply(lower, 0, j)
         add_and_round(lower, 1)
-        lows = [scale_lower(0, j) for j in range(PX_TILES)]
-        turned_0 = [turn_and_add(0, j, lows[j]) for j in range(PX_TILES)]
-        quantise_and_multiply(lower, 1)
+        quantise(lower, 1)
+        for first in range(0, PX_TILES, 2):
+            pair = (first, first + 1)
+            lows = [scale_lower(0, j) for j in pair]
+            for j in pair:
+                multiply(lower, 1, j)
+            for j in pair:
+                turn_into(turned_0[j], lows[j - first], False)
+        turned_1 = [combine_and_turn(1, j) for j in range(PX_TILES)]
         for j in range(PX_TILES):
             store_pixels(0, j, turned_0[j], False)
-        turned_1 = [combine_and_turn(1, j) for j in range(PX_TILES)]
         for j in range(PX_TILES):
             store_pixels(1, j, turned_1[j], j % 2 == 1)

from contextlib import ExitStack

import concourse.mybir as mybir
from concourse.masks import make_identity

F32 = mybir.dt.float32
BF16 = mybir.dt.bfloat16
U32 = mybir.dt.uint32
U8 = mybir.dt.uint8
E4M3X4 = mybir.dt.float8_e4m3fn_x4
E5M2X4 = mybir.dt.float8_e5m2_x4
ALU = mybir.AluOpType
ACT = mybir.ActivationFunctionType

P = 128
PACK = 4
BATCH = 2
PIXELS = 512
C_IN = 512
UPPER_PASSES = 2
PASSES = 3
UNITS = PASSES * PACK
PX_TILES = PIXELS // P
C_TILES = C_IN // P
VALUES = BATCH * PIXELS
LOAD_AHEAD = 8

FIRST_HALF_STEP = 6
STEPS_PER_HALF = 2
HALVES_IN_LOOP = 3
VECTOR_COPIES = 2
WEIGHT_EVERY = 2
WEIGHT_LOAD_UNIT = 3
WEIGHT_REGROUP_STEP = 4
WEIGHT_QUANTISE_STEP = 6
ATTENTION_STEP = 3
LATER_PASSES = (1, 2)

ROW_GAMMA = 0
ROW_BETA = ROW_GAMMA + UNITS
ROW_ATT = ROW_BETA + UNITS
ROW_F32 = 64
ROW_MEAN = ROW_F32
ROW_RSTD = ROW_MEAN + UNITS

FLOPS = 2 * UNITS * P * C_IN * VALUES
BYTES = (
    UNITS * P * VALUES * (4 + 2)
    + UNITS * P * C_IN * 2
    + UNITS * P * (2 + 2 + 4 + 4)
    + 2 * VALUES * 2
    + C_IN * VALUES * 4
)


def by_fours_rows(ap):
    return ap.rearrange("p t (c i) -> p c t i", i=PACK)


def by_fours_words(ap):
    return ap.rearrange("p (c i) t -> p c t i", i=PACK)


def weight_pass_at(distance):
    c, rest = divmod(distance, WEIGHT_EVERY)
    return c if rest == 0 and 0 <= c < PASSES else None


def tile_gnn_t_v_kernel(
    tc, p_nodes, h_nodes, f_nodes, xp, h_att, Wu, Wl, gamma_u, beta_u, gamma_l, beta_l, y, mean, rstd, grad_out, out
):
    nc = tc.nc
    with ExitStack() as ctx:
        keep = ctx.enter_context(tc.tile_pool(name="keep", bufs=1))
        loads = ctx.enter_context(tc.tile_pool(name="loads", bufs=LOAD_AHEAD))
        work = ctx.enter_context(tc.tile_pool(name="work", bufs=2))
        psum = ctx.enter_context(tc.psum_pool(name="psum", bufs=4))
        ctx.enter_context(tc.manual_schedule())

        rows_f32 = keep.tile([P, P], F32)
        rows_bf16 = keep.tile([P, P], BF16)
        att_rows = keep.tile([P, P], BF16)
        nc.gpsimd.memset(rows_f32[:], 0.0)
        nc.gpsimd.memset(rows_bf16[:], 0.0)
        addend = keep.tile([P, UNITS, 2], F32)
        nc.gpsimd.memset(addend[:], 0.0)
        upper_units = UPPER_PASSES * PACK
        w_views = [Wu.rearrange("(c t p) n -> c p t n", t=PACK, p=P)[c] for c in range(UPPER_PASSES)]
        w_views.append(Wl.rearrange("(t p) n -> p t n", p=P))
        w_raws = {}

        def load_weights(c):
            w_raw = keep.tile([P, PACK, C_IN], BF16, name="w_raw%d" % c)
            nc.sync.dma_start(out=w_raw[:], in_=w_views[c])
            w_raws[c] = w_raw

        load_weights(0)
        nc.sync.dma_start(out=rows_f32[0:UNITS, :], in_=mean.rearrange("(r q) -> r q", q=P))
        nc.sync.dma_start(out=rows_f32[UNITS : 2 * UNITS, :], in_=rstd.rearrange("(r q) -> r q", q=P))
        for vec_u, vec_l, row in ((gamma_u, gamma_l, 0), (beta_u, beta_l, UNITS)):
            nc.sync.dma_start(out=rows_bf16[row : row + upper_units, :], in_=vec_u.rearrange("(r q) -> r q", q=P))
            nc.sync.dma_start(
                out=rows_bf16[row + upper_units : row + UNITS, :], in_=vec_l.rearrange("(r q) -> r q", q=P)
            )
        identity = keep.tile([P, P], F32)
        make_identity(nc, identity[:])
        identity_bf16 = keep.tile([P, P], BF16)
        make_identity(nc, identity_bf16[:])
        nc.gpsimd.memset(att_rows[:], 0.0)

        y_view = y.rearrange("b (u p) h w -> u p b (h w)", p=P)
        g_view = grad_out.rearrange("n b (v p) h w -> n v p b (h w)", p=P)
        y_units = {}
        g_units = {}

        def load_unit(u):
            y_unit = loads.tile([P, BATCH, PIXELS], F32)
            nc.sync.dma_start(out=y_unit[:], in_=y_view[u])
            g_unit = loads.tile([P, BATCH, PIXELS], BF16)
            nc.sync.dma_start(out=g_unit[:], in_=g_view[1 + u // 2, u % 2])
            y_units[u] = y_unit
            g_units[u] = g_unit

        for u in range(LOAD_AHEAD):
            load_unit(u)
            if u == 1:
                nc.sync.dma_start(
                    out=att_rows[0 : 2 * BATCH * PX_TILES, :],
                    in_=h_att[1:3].rearrange("i b o (j h) w -> (i b o j) (h w)", j=PX_TILES),
                )
            if weight_pass_at(u - WEIGHT_LOAD_UNIT) in LATER_PASSES:
                load_weights(weight_pass_at(u - WEIGHT_LOAD_UNIT))

        w_codes = keep.tile([P, PASSES, C_IN], U32, align_bytes=64)
        w_scales = keep.tile([P, PASSES, C_IN], U8, align_bytes=64)
        w_words = {}

        def regroup_weights(c, by_vector=False):
            w_word = work.tile([P, C_IN, PACK], BF16, align_bytes=64)
            if by_vector:
                nc.vector.tensor_copy(out=by_fours_words(w_word[:]), in_=by_fours_rows(w_raws[c][:]))
            else:
                nc.scalar.copy(out=by_fours_words(w_word[:]), in_=by_fours_rows(w_raws[c][:]))
            w_words[c] = w_word

        def quantise_weights(c):
            nc.vector.quantize_mx(
                out=w_codes[:, c, :].bitcast(E4M3X4),
                scales=w_scales[:, c, :],
                in_=w_words[c][:].rearrange("p n t -> p (n t)"),
            )

        regroup_weights(0, True)
        quantise_weights(0)

        f32_psum = psum.tile([P, C_IN], F32, tag="b")
        nc.tensor.transpose(f32_psum[:, 0:P], rows_f32[:], identity[:])
        bf16_psum = psum.tile([P, 2 * C_IN], BF16, tag="b")
        nc.tensor.transpose(bf16_psum[:, 0:P], rows_bf16[:], identity_bf16[:])
        cols_f32 = keep.tile([P, 2 * UNITS], F32)
        nc.vector.tensor_copy(out=cols_f32[:], in_=f32_psum[:, 0 : 2 * UNITS])
        mean_c = cols_f32[:, 0:UNITS]
        rstd_c = cols_f32[:, UNITS : 2 * UNITS]
        rstd_sq = keep.tile([P, UNITS], F32)
        nc.vector.tensor_tensor(out=rstd_sq[:], in0=rstd_c, in1=rstd_c, op=ALU.mult)
        gamma = bf16_psum[:, 0:UNITS]
        beta = bf16_psum[:, UNITS : 2 * UNITS]
        att_cols = keep.tile([P, 2 * BATCH * PX_TILES], F32)

        def turn_attention():
            att_psum = psum.tile([P, 2 * C_IN], BF16, tag="b")
            nc.tensor.transpose(att_psum[:, 0:P], att_rows[:], identity_bf16[:])
            nc.scalar.copy(out=att_cols[:], in_=att_psum[:, 0 : 2 * BATCH * PX_TILES])

        def att(i, b, j):
            r = (i * BATCH + b) * PX_TILES + j
            return att_cols[:, r : r + 1]

        z_slope = keep.tile([P, UNITS], F32)
        nc.vector.tensor_tensor(out=z_slope[:], in0=rstd_c, in1=gamma, op=ALU.mult)
        mean_z_slope = keep.tile([P, UNITS], F32)
        nc.vector.tensor_tensor(out=mean_z_slope[:], in0=mean_c, in1=z_slope[:], op=ALU.mult)
        e_scale = keep.tile([P, UNITS], F32)
        nc.vector.tensor_scalar(out=e_scale[:], in0=z_slope[:], scalar1=0.5, scalar2=None, op0=ALU.mult)
        z_thresh = keep.tile([P, UNITS], F32)
        nc.vector.tensor_tensor(out=z_thresh[:], in0=mean_z_slope[:], in1=beta, op=ALU.subtract)
        k_line = keep.tile([P, UNITS, 2], F32)

        sum_cm = keep.tile([P, UNITS], F32)
        sum_e = keep.tile([P, UNITS], F32)
        line = keep.tile([P, UNITS, 2], F32)
        relu_units = {}
        masked_units = {}
        e_passes = {}
        corr_passes = {}

        def find_relu(u):
            one = slice(u, u + 1)
            relu_on = work.tile([P, BATCH, PIXELS], BF16)
            nc.vector.tensor_scalar(
                out=relu_on[:], in0=y_units[u][:], scalar1=z_slope[:, one], scalar2=z_thresh[:, one],
                op0=ALU.mult, op1=ALU.is_gt,
            )
            relu_units[u] = relu_on

        def mask_gradient(u):
            masked = work.tile([P, BATCH, PIXELS], BF16, bufs=3)
            nc.vector.tensor_tensor(out=masked[:], in0=relu_units[u][:], in1=g_units[u][:], op=ALU.mult)
            masked_units[u] = masked

        def sum_centred(u):
            one = slice(u, u + 1)
            product = work.tile([P, BATCH, PIXELS], BF16)
            nc.vector.scalar_tensor_tensor(
                out=product[:], in0=y_units[u][:], scalar=mean_c[:, one], in1=masked_units[u][:],
                op0=ALU.subtract, op1=ALU.mult, accum_out=sum_cm[:, one],
            )

        def scale_gradient(u):
            c, t = divmod(u, PACK)
            one = slice(u, u + 1)
            if t == 0:
                e_pass = work.tile([P, PACK, BATCH, PIXELS], F32)
                e_passes[c] = e_pass
            nc.scalar.activation(
                out=e_passes[c][:, t], in_=masked_units[u][:], func=ACT.Copy,
                scale=e_scale[:, one], accum_out=sum_e[:, one],
            )
            nc.scalar.activation(out=addend[:, u, 1:2], in_=sum_e[:, one], func=ACT.Copy, scale=-1.0 / VALUES)

        def line_of_correction(u):
            nc.vector.scalar_tensor_tensor(
                out=line[:, u, :], in0=k_line[:, u, :], scalar=sum_cm[:, u : u + 1], in1=addend[:, u, :],
                op0=ALU.mult, op1=ALU.add,
            )

        def correction(u):
            c, t = divmod(u, PACK)
            if t == 0:
                corr_pass = work.tile([P, PACK, BATCH, PIXELS], F32)
                corr_passes[c] = corr_pass
            nc.scalar.activation(
                out=corr_passes[c][:, t], in_=y_units[u][:], func=ACT.Identity,
                scale=line[:, u, 0:1], bias=line[:, u, 1:2],
            )

        dy_codes = keep.tile([P, PASSES, BATCH, PIXELS], U32, align_bytes=64)
        dy_scales = keep.tile([P, PASSES, BATCH, PIXELS], U8, align_bytes=64)
        dy_words = {}
        sums = {}

        def add_and_round(c, b):
            dy_word = work.tile([P, PIXELS, PACK], BF16, align_bytes=64)
            nc.vector.tensor_tensor(
                out=by_fours_words(dy_word[:]),
                in0=by_fours_rows(e_passes[c][:, :, b, :]),
                in1=by_fours_rows(corr_passes[c][:, :, b, :]),
                op=ALU.add,
            )
            dy_words[(c, b)] = dy_word

        def quantise(c, b):
            nc.vector.quantize_mx(
                out=dy_codes[:, c, b, :].bitcast(E5M2X4),
                scales=dy_scales[:, c, b, :],
                in_=dy_words[(c, b)][:].rearrange("p w t -> p (w t)"),
            )

        def multiply(c, b, j):
            opens = c == 0 or c == UPPER_PASSES
            closes = c == UPPER_PASSES - 1 or c == PASSES - 1
            px = slice(j * P, (j + 1) * P)
            if opens:
                acc = psum.tile([P, C_IN], F32, tag="a" if (c == 0 and b == 0) else "b")
                sums[(b, j)] = acc
            nc.tensor.matmul_mx(
                out=sums[(b, j)][:],
                lhsT=dy_codes[:, c, b, px].bitcast(E5M2X4),
                lhsT_scale=dy_scales[:, c, b, px],
                rhs=w_codes[:, c, :].bitcast(E4M3X4),
                rhs_scale=w_scales[:, c, :],
                start=opens,
                stop=closes,
            )

        def quantise_and_multiply(c, b):
            quantise(c, b)
            for j in range(PX_TILES):
                multiply(c, b, j)

        upper = keep.tile([P, BATCH, PX_TILES, C_IN], F32)

        def keep_upper(b):
            for j in range(PX_TILES):
                nc.scalar.activation(out=upper[:, b, j, :], in_=sums[(b, j)][:], func=ACT.Copy, scale=att(0, b, j))

        out_view = out.rearrange("b (m p) (j h) w -> b j p m (h w)", p=P, j=PX_TILES)

        def combine_and_turn(b, j):
            total = work.tile([P, C_IN], F32, bufs=4)
            nc.vector.scalar_tensor_tensor(
                out=total[:], in0=sums[(b, j)][:], scalar=att(1, b, j), in1=upper[:, b, j, :],
                op0=ALU.mult, op1=ALU.add,
            )
            turned = psum.tile([P, C_TILES, P], F32, tag="b")
            for m in range(C_TILES):
                nc.tensor.transpose(turned[:, m, :], total[:, m * P : (m + 1) * P], identity[:])
            return turned

        def scale_lower(b, j):
            low = work.tile([P, C_IN], F32, bufs=4)
            nc.scalar.activation(out=low[:], in_=sums[(b, j)][:], func=ACT.Copy, scale=att(1, b, j))
            return low

        def turn_into(turned, source, first):
            for m in range(C_TILES):
                nc.tensor.matmul(
                    turned[:, m, :], lhsT=source[:, m * P : (m + 1) * P], rhs=identity[:], is_transpose=True,
                    start=first and m == 0, stop=(not first) and m == C_TILES - 1,
                )

        def store_pixels(b, j, turned, by_vector):
            result = work.tile([P, C_TILES, P], F32, bufs=len(tiles))
            if by_vector:
                nc.vector.tensor_copy(out=result[:], in_=turned[:])
            else:
                nc.scalar.copy(out=result[:], in_=turned[:])
            nc.sync.dma_start(out=out_view[b, j], in_=result[:])

        find_relu(0)
        nc.vector.scalar_tensor_tensor(
            out=k_line[:, :, 0], in0=rstd_sq[:], scalar=-1.0 / VALUES, in1=e_scale[:], op0=ALU.mult, op1=ALU.mult
        )
        nc.vector.scalar_tensor_tensor(
            out=k_line[:, :, 1], in0=k_line[:, :, 0], scalar=-1.0, in1=mean_c, op0=ALU.mult, op1=ALU.mult
        )
        for i in range(UNITS + 1):
            half, odd_step = divmod(i - FIRST_HALF_STEP, STEPS_PER_HALF)
            finishing = odd_step == 0 and 0 <= half < HALVES_IN_LOOP
            c_done, b_done = divmod(half, BATCH)
            if finishing:
                add_and_round(c_done, b_done)
            if i < UNITS:
                mask_gradient(i)
            if i >= 1:
                line_of_correction(i - 1)
            if i + 1 < UNITS:
                find_relu(i + 1)
            if i < UNITS:
                sum_centred(i)
            if weight_pass_at(i - WEIGHT_QUANTISE_STEP) in LATER_PASSES:
                quantise_weights(weight_pass_at(i - WEIGHT_QUANTISE_STEP))
            if finishing:
                quantise_and_multiply(c_done, b_done)
            if i < UNITS:
                scale_gradient(i)
            if i >= 1:
                correction(i - 1)
                if i - 1 + LOAD_AHEAD < UNITS:
                    load_unit(i - 1 + LOAD_AHEAD)
            if weight_pass_at(i - WEIGHT_REGROUP_STEP) in LATER_PASSES:
                regroup_weights(weight_pass_at(i - WEIGHT_REGROUP_STEP))
            if i == ATTENTION_STEP:
                turn_attention()

        lower = PASSES - 1
        tiles = [(b, j) for b in range(BATCH) for j in range(PX_TILES)]
        keep_upper(0)
        turned_0 = []
        for j in range(PX_TILES):
            turned = psum.tile([P, C_TILES, P], F32, tag="a")
            turn_into(turned, upper[:, 0, j, :], True)
            turned_0.append(turned)
        add_and_round(UPPER_PASSES - 1, 1)
        add_and_round(lower, 0)
        quantise_and_multiply(UPPER_PASSES - 1, 1)
        quantise(lower, 0)
        keep_upper(1)
        for j in range(PX_TILES):
            multiply(lower, 0, j)
        add_and_round(lower, 1)
        quantise(lower, 1)
        for first in range(0, PX_TILES, 2):
            pair = (first, first + 1)
            lows = [scale_lower(0, j) for j in pair]
            for j in pair:
                multiply(lower, 1, j)
            for j in pair:
                turn_into(turned_0[j], lows[j - first], False)
        turned_1 = [combine_and_turn(1, j) for j in range(PX_TILES)]
        for j in range(PX_TILES):
            store_pixels(0, j, turned_0[j], False)
        for j in range(PX_TILES):
            store_pixels(1, j, turned_1[j], j % 2 == 1)
